import numpy as np
import ml_dtypes

BF16 = ml_dtypes.bfloat16


def bf(x):
    return np.asarray(x, np.float32).astype(BF16)


def f32(x):
    return np.asarray(x, np.float32)


def f64(x):
    return np.asarray(x).astype(np.float64)


def striped(idx):
    return np.tile(idx.reshape(-1, 16).T, (8, 1))


Q, S, N, K, XY = 256, 256, 256, 4, 2
CLASS_COST, POLY_COST, GIOU_COST, EPS = 1.0, 5.0, 1.0, 1e-6


def setup_inputs():
    return {"logits": f32(4.0 * np.random.standard_normal((Q, S))), "pred_poly": f32(0.25 + 0.5 * np.random.random_sample((Q, K * XY))), "tgt_poly": f32(0.25 + 0.5 * np.random.random_sample((K * XY, N))), "offs": striped(np.random.permutation(np.tile(np.arange(S), 2))[:N])}


def reference(logits, pred_poly, tgt_poly, offs):
    idx = offs[:16].T.reshape(-1)
    z = f64(logits)
    e = np.exp(z - z.max(axis=1, keepdims=True))
    prob = e / e.sum(axis=1, keepdims=True)
    p = f64(pred_poly).reshape(Q, K, XY, 1)
    t = f64(tgt_poly).reshape(1, K, XY, N)
    fwd = np.abs(p - t).sum(axis=(1, 2)) / (K * XY)
    rev = np.abs(p - t[:, ::-1]).sum(axis=(1, 2)) / (K * XY)
    poly = np.minimum(fwd, rev)
    alo, ahi = p.min(axis=1), p.max(axis=1)
    blo, bhi = t.min(axis=1), t.max(axis=1)
    area1 = (ahi - alo).prod(axis=1)
    area2 = (bhi - blo).prod(axis=1)
    inter = np.maximum(np.minimum(ahi, bhi) - np.maximum(alo, blo), 0.0).prod(axis=1)
    union = area1 + area2 - inter
    hull = (np.maximum(ahi, bhi) - np.minimum(alo, blo)).prod(axis=1)
    giou = inter / np.maximum(union, EPS) - (hull - union) / np.maximum(hull, EPS)
    return -CLASS_COST * prob[:, idx] + POLY_COST * poly - GIOU_COST * giou

@@ -1,0 +1,167 @@
+import concourse.mybir as mybir
+
+F32 = mybir.dt.float32
+U16 = mybir.dt.uint16
+ALU = mybir.AluOpType
+FN = mybir.ActivationFunctionType
+X = mybir.AxisListType.X
+
+P = 128
+Q, S, N = 256, 256, 256
+K, XY = 4, 2
+BLOCKS = Q // P
+EPS = 1e-6
+
+
+def tile_hungarianmatcherpolyline_kernel(tc, logits, pred_poly, tgt_poly, offs, out):
+    nc = tc.nc
+    with tc.tile_pool(name="held", bufs=1) as held, tc.psum_pool(name="psum", bufs=1) as psum:
+        offsets = held.tile([P, N // 16], U16, name="offsets")
+        nc.sync.dma_start(offsets[:], offs)
+
+        pred = held.tile([P, BLOCKS, K, XY], F32, name="pred")
+        nc.sync.dma_start(pred[:], pred_poly.rearrange("(b p) (k d) -> p b k d", p=P, d=XY))
+
+        tgt_rows = held.tile([K * XY, N], F32, name="tgt_rows")
+        nc.scalar.dma_start(tgt_rows[:], tgt_poly)
+
+        scores = []
+        for b in range(BLOCKS):
+            block = held.tile([P, S], F32, name=f"scores{b}")
+            nc.scalar.dma_start(block[:], logits[b * P : (b + 1) * P, :])
+            scores.append(block)
+
+        tgt = held.tile([P, K, XY * N], F32, name="tgt")
+        for k, queue in ((0, nc.sync), (3, nc.scalar), (1, nc.sync), (2, nc.scalar)):
+            rows = tgt_poly[k * XY : (k + 1) * XY, :].rearrange("r j -> (r j)")
+            queue.dma_start(tgt[:, k, :], rows.partition_broadcast(P))
+
+        def tgt_row(k, d):
+            return tgt[:, k, d * N : (d + 1) * N]
+
+        by_coord = pred[:].rearrange("p b k d -> p b d k")
+        a_hi = held.tile([P, BLOCKS, XY], F32, name="a_hi")
+        a_lo = held.tile([P, BLOCKS, XY], F32, name="a_lo")
+        nc.vector.tensor_reduce(out=a_hi[:], in_=by_coord, axis=X, op=ALU.max)
+        nc.vector.tensor_reduce(out=a_lo[:], in_=by_coord, axis=X, op=ALU.min)
+        a_side = held.tile([P, BLOCKS, XY], F32, name="a_side")
+        nc.vector.tensor_sub(a_side[:], a_hi[:], a_lo[:])
+        area1 = held.tile([P, BLOCKS], F32, name="area1")
+        nc.vector.tensor_mul(area1[:], a_side[:, :, 0], a_side[:, :, 1])
+        pred_sum = held.tile([P, BLOCKS], F32, name="pred_sum")
+        nc.vector.tensor_reduce(
+            out=pred_sum[:], in_=pred[:].rearrange("p b k d -> p b (k d)"), axis=X, op=ALU.add
+        )
+        pred_term = held.tile([P, BLOCKS], F32, name="pred_term")
+        nc.vector.tensor_scalar_mul(pred_term[:], pred_sum[:], -0.625)
+
+        neg_prob = []
+        for b in range(BLOCKS):
+            neg_max = held.tile([P, 1], F32, name=f"neg_max{b}")
+            nc.vector.tensor_reduce(out=neg_max[:], in_=scores[b][:], axis=X, op=ALU.max, negate=True)
+            expd = held.tile([P, S], F32, name=f"expd{b}")
+            total = held.tile([P, 1], F32, name=f"total{b}")
+            nc.scalar.activation(
+                out=expd[:], in_=scores[b][:], func=FN.Exp, bias=neg_max[:], scale=1.0, accum_out=total[:]
+            )
+            neg_total = held.tile([P, 1], F32, name=f"neg_total{b}")
+            nc.vector.tensor_scalar_mul(neg_total[:], total[:], -1.0)
+            neg_inv = held.tile([P, 1], F32, name=f"neg_inv{b}")
+            nc.vector.reciprocal(neg_inv[:], neg_total[:])
+            window = held.tile([P, S], F32, name=f"neg_prob{b}")
+            nc.scalar.activation(out=window[:], in_=expd[:], func=FN.Copy, scale=neg_inv[:])
+            neg_prob.append(window)
+
+        minus_half = held.tile([K * XY, P], F32, name="minus_half")
+        nc.vector.memset(minus_half[:], -0.5)
+        tgt_term = psum.tile([P, N], F32, name="tgt_term")
+        nc.tensor.matmul(tgt_term[:], minus_half[:], tgt_rows[:], start=True, stop=True)
+
+        sums = [[tgt_term, tgt_term] for b in range(BLOCKS)]
+
+        def add_point(k):
+            for d in range(XY):
+                for b in range(BLOCKS):
+                    for order, partner in enumerate((k, K - 1 - k)):
+                        longer = held.tile([P, N], F32, name=f"sum{b}{order}{k}{d}")
+                        nc.vector.scalar_tensor_tensor(
+                            out=longer[:],
+                            in0=tgt_row(partner, d),
+                            scalar=pred[:, b, k, d : d + 1],
+                            in1=sums[b][order][:],
+                            op0=ALU.max,
+                            op1=ALU.add,
+                        )
+                        sums[b][order] = longer
+
+        add_point(0)
+        add_point(3)
+
+        b_hi = held.tile([P, XY * N], F32, name="b_hi")
+        b_lo = held.tile([P, XY * N], F32, name="b_lo")
+        for edge, op, label in ((b_hi, ALU.max, "hi"), (b_lo, ALU.min, "lo")):
+            halves = held.tile([P, 2, XY * N], F32, name=f"halves_{label}")
+            nc.vector.tensor_tensor(halves[:], tgt[:, 0:2, :], tgt[:, 2:4, :], op)
+            nc.vector.tensor_tensor(edge[:], halves[:, 0, :], halves[:, 1, :], op)
+        b_side = held.tile([P, XY * N], F32, name="b_side")
+        nc.vector.tensor_sub(b_side[:], b_hi[:], b_lo[:])
+        area2 = held.tile([P, N], F32, name="area2")
+        nc.vector.tensor_mul(area2[:], b_side[:, 0:N], b_side[:, N : 2 * N])
+
+        tops = []
+        inverses = []
+        for b in range(BLOCKS):
+            overlap = held.tile([P, XY * N], F32, name=f"overlap{b}")
+            extent = held.tile([P, XY * N], F32, name=f"extent{b}")
+            for d in range(XY):
+                cols = slice(d * N, (d + 1) * N)
+                hi, lo = a_hi[:, b, d : d + 1], a_lo[:, b, d : d + 1]
+                above = held.tile([P, N], F32, name=f"above{b}{d}")
+                nc.scalar.activation(out=above[:], in_=b_hi[:, cols], func=FN.Relu, bias=hi, scale=-1.0)
+                lost = held.tile([P, N], F32, name=f"lost{b}{d}")
+                nc.vector.scalar_tensor_tensor(
+                    out=lost[:], in0=b_lo[:, cols], scalar=lo, in1=above[:], op0=ALU.max, op1=ALU.add
+                )
+                nc.scalar.activation(out=overlap[:, cols], in_=lost[:], func=FN.Relu, bias=hi, scale=-1.0)
+                nc.vector.scalar_tensor_tensor(
+                    out=extent[:, cols], in0=lost[:], scalar=lo, in1=b_side[:, cols],
+                    op0=ALU.subtract, op1=ALU.add,
+                )
+            top = held.tile([P, 2 * N], F32, name=f"top{b}")
+            bottom = held.tile([P, 2 * N], F32, name=f"bottom{b}")
+            inter, union, hull = top[:, 0:N], bottom[:, 0:N], bottom[:, N : 2 * N]
+            nc.vector.tensor_mul(inter, overlap[:, 0:N], overlap[:, N : 2 * N])
+            nc.vector.tensor_mul(hull, extent[:, 0:N], extent[:, N : 2 * N])
+            nc.vector.scalar_tensor_tensor(
+                out=union, in0=area2[:], scalar=area1[:, b : b + 1], in1=inter, op0=ALU.add, op1=ALU.subtract
+            )
+            nc.vector.tensor_sub(top[:, N : 2 * N], hull, union)
+            floored = held.tile([P, 2 * N], F32, name=f"floored{b}")
+            nc.vector.tensor_scalar_max(floored[:], bottom[:], EPS)
+            logd = held.tile([P, 2 * N], F32, name=f"logd{b}")
+            nc.scalar.activation(out=logd[:], in_=floored[:], func=FN.Ln)
+            inverse = held.tile([P, 2 * N], F32, name=f"inverse{b}")
+            nc.scalar.activation(out=inverse[:], in_=logd[:], func=FN.Exp, scale=-1.0)
+            tops.append(top)
+            inverses.append(inverse)
+
+        add_point(1)
+        add_point(2)
+
+        for b in range(BLOCKS):
+            best = held.tile([P, N], F32, name=f"best{b}")
+            nc.vector.tensor_tensor(best[:], sums[b][0][:], sums[b][1][:], ALU.min)
+            ratios = held.tile([P, 2 * N], F32, name=f"ratios{b}")
+            nc.vector.tensor_mul(ratios[:], tops[b][:], inverses[b][:])
+            partial = held.tile([P, N], F32, name=f"partial{b}")
+            nc.vector.scalar_tensor_tensor(
+                out=partial[:], in0=best[:], scalar=1.25, in1=ratios[:, 0:N], op0=ALU.mult, op1=ALU.subtract
+            )
+            others = held.tile([P, N], F32, name=f"others{b}")
+            nc.vector.scalar_tensor_tensor(
+                out=others[:], in0=partial[:], scalar=pred_term[:, b : b + 1], in1=ratios[:, N : 2 * N],
+                op0=ALU.add, op1=ALU.add,
+            )
+            cost = held.tile([P, N], F32, name=f"cost{b}")
+            nc.vector.tensor_tensor(cost[:], neg_prob[b][:].indirect(offsets[:]), others[:], ALU.add)
+            nc.sync.dma_start(out[b * P : (b + 1) * P, :], cost[:])

@@ -1,4 +1,5 @@
 import concourse.mybir as mybir
+from concourse.masks import make_identity
 
 F32 = mybir.dt.float32
 U16 = mybir.dt.uint16
@@ -10,7 +11,10 @@ P = 128
 Q, S, N = 256, 256, 256
 K, XY = 4, 2
 BLOCKS = Q // P
+HALVES = N // P
 EPS = 1e-6
+LO, HI, SIDE, AREA = 0, 1, 2, 3
+STATS = 4
 
 
 def tile_hungarianmatcherpolyline_kernel(tc, logits, pred_poly, tgt_poly, offs, out):
@@ -22,8 +26,9 @@ def tile_hungarianmatcherpolyline_kernel(tc, logits, pred_poly, tgt_poly, offs, 
         pred = held.tile([P, BLOCKS, K, XY], F32, name="pred")
         nc.sync.dma_start(pred[:], pred_poly.rearrange("(b p) (k d) -> p b k d", p=P, d=XY))
 
-        tgt_rows = held.tile([K * XY, N], F32, name="tgt_rows")
-        nc.scalar.dma_start(tgt_rows[:], tgt_poly)
+        tgt_rows = held.tile([P, N], F32, name="tgt_rows")
+        nc.gpsimd.memset(tgt_rows[:], 0.0)
+        nc.scalar.dma_start(tgt_rows[0 : K * XY, :], tgt_poly)
 
         scores = []
         for b in range(BLOCKS):
@@ -38,6 +43,15 @@ def tile_hungarianmatcherpolyline_kernel(tc, logits, pred_poly, tgt_poly, offs, 
 
         def tgt_row(k, d):
             return tgt[:, k, d * N : (d + 1) * N]
+
+        ident = held.tile([P, P], F32, name="ident")
+        make_identity(nc, ident[:])
+        pick = held.tile([P, STATS, P], F32, name="pick")
+        nc.vector.tensor_copy(pick[:], ident[:, 0:STATS].unsqueeze(2).to_broadcast([P, STATS, P]))
+        minus_half = held.tile([P, P], F32, name="minus_half")
+        nc.gpsimd.memset(minus_half[:], -0.5)
+        stat_rows = held.tile([P, XY * N], F32, name="stat_rows")
+        nc.gpsimd.memset(stat_rows[:], 0.0)
 
         by_coord = pred[:].rearrange("p b k d -> p b d k")
         a_hi = held.tile([P, BLOCKS, XY], F32, name="a_hi")
@@ -72,10 +86,36 @@ def tile_hungarianmatcherpolyline_kernel(tc, logits, pred_poly, tgt_poly, offs, 
             nc.scalar.activation(out=window[:], in_=expd[:], func=FN.Copy, scale=neg_inv[:])
             neg_prob.append(window)
 
-        minus_half = held.tile([K * XY, P], F32, name="minus_half")
-        nc.vector.memset(minus_half[:], -0.5)
         tgt_term = psum.tile([P, N], F32, name="tgt_term")
         nc.tensor.matmul(tgt_term[:], minus_half[:], tgt_rows[:], start=True, stop=True)
+
+        tgt_t = psum.tile([P, HALVES, P], F32, name="tgt_t")
+        for h in range(HALVES):
+            nc.tensor.transpose(tgt_t[:, h, :], tgt_rows[:, h * P : (h + 1) * P], ident[:])
+        points_last = tgt_t[:, :, 0 : K * XY].rearrange("p h (k d) -> p d h k", d=XY)
+        stat = held.tile([P, XY, HALVES, STATS], F32, name="stat")
+        nc.vector.tensor_reduce(out=stat[:, :, :, LO], in_=points_last, axis=X, op=ALU.min)
+        nc.vector.tensor_reduce(out=stat[:, :, :, HI], in_=points_last, axis=X, op=ALU.max)
+        nc.vector.tensor_sub(stat[:, :, :, SIDE], stat[:, :, :, HI], stat[:, :, :, LO])
+        nc.vector.tensor_mul(
+            stat[:, :, :, AREA],
+            stat[:, 0:1, :, SIDE].to_broadcast([P, XY, HALVES]),
+            stat[:, 1:2, :, SIDE].to_broadcast([P, XY, HALVES]),
+        )
+        stat_t = psum.tile([P, XY * N], F32, name="stat_t")
+        for d in range(XY):
+            for h in range(HALVES):
+                first = d * N + h * P
+                nc.tensor.transpose(stat_t[0:STATS, first : first + P], stat[:, d, h, :], ident[:])
+        nc.scalar.copy(stat_rows[0:STATS, :], stat_t[0:STATS, :])
+        b_hi = psum.tile([P, XY * N], F32, name="b_hi")
+        b_lo = psum.tile([P, XY * N], F32, name="b_lo")
+        b_side = psum.tile([P, XY * N], F32, name="b_side")
+        area2 = psum.tile([P, N], F32, name="area2")
+        nc.tensor.matmul(b_hi[:], pick[:, HI, :], stat_rows[:], start=True, stop=True)
+        nc.tensor.matmul(b_lo[:], pick[:, LO, :], stat_rows[:], start=True, stop=True)
+        nc.tensor.matmul(b_side[:], pick[:, SIDE, :], stat_rows[:], start=True, stop=True)
+        nc.tensor.matmul(area2[:], pick[:, AREA, :], stat_rows[:, 0:N], start=True, stop=True)
 
         sums = [[tgt_term, tgt_term] for b in range(BLOCKS)]
 
@@ -96,17 +136,6 @@ def tile_hungarianmatcherpolyline_kernel(tc, logits, pred_poly, tgt_poly, offs, 
 
         add_point(0)
         add_point(3)
-
-        b_hi = held.tile([P, XY * N], F32, name="b_hi")
-        b_lo = held.tile([P, XY * N], F32, name="b_lo")
-        for edge, op, label in ((b_hi, ALU.max, "hi"), (b_lo, ALU.min, "lo")):
-            halves = held.tile([P, 2, XY * N], F32, name=f"halves_{label}")
-            nc.vector.tensor_tensor(halves[:], tgt[:, 0:2, :], tgt[:, 2:4, :], op)
-            nc.vector.tensor_tensor(edge[:], halves[:, 0, :], halves[:, 1, :], op)
-        b_side = held.tile([P, XY * N], F32, name="b_side")
-        nc.vector.tensor_sub(b_side[:], b_hi[:], b_lo[:])
-        area2 = held.tile([P, N], F32, name="area2")
-        nc.vector.tensor_mul(area2[:], b_side[:, 0:N], b_side[:, N : 2 * N])
 
         tops = []
         inverses = []

@@ -15,182 +15,245 @@ HALVES = N // P
 EPS = 1e-6
 LO, HI, SIDE, AREA = 0, 1, 2, 3
 STATS = 4
+OFFLOADED = 3
 
 
 def tile_hungarianmatcherpolyline_kernel(tc, logits, pred_poly, tgt_poly, offs, out):
     nc = tc.nc
     with tc.tile_pool(name="held", bufs=1) as held, tc.psum_pool(name="psum", bufs=1) as psum:
-        offsets = held.tile([P, N // 16], U16, name="offsets")
-        nc.sync.dma_start(offsets[:], offs)
+        tgt_rows = held.tile([K * XY, N], F32, name="tgt_rows")
+        nc.scalar.dma_start(tgt_rows[:], tgt_poly)
 
         pred = held.tile([P, BLOCKS, K, XY], F32, name="pred")
-        nc.sync.dma_start(pred[:], pred_poly.rearrange("(b p) (k d) -> p b k d", p=P, d=XY))
-
-        tgt_rows = held.tile([P, N], F32, name="tgt_rows")
-        nc.gpsimd.memset(tgt_rows[:], 0.0)
-        nc.scalar.dma_start(tgt_rows[0 : K * XY, :], tgt_poly)
-
-        scores = []
-        for b in range(BLOCKS):
-            block = held.tile([P, S], F32, name=f"scores{b}")
-            nc.scalar.dma_start(block[:], logits[b * P : (b + 1) * P, :])
-            scores.append(block)
+        nc.sync.dma_start(pred[:], pred_poly.rearrange("(p b) (k d) -> p b k d", b=BLOCKS, d=XY))
 
         tgt = held.tile([P, K, XY * N], F32, name="tgt")
-        for k, queue in ((0, nc.sync), (3, nc.scalar), (1, nc.sync), (2, nc.scalar)):
-            rows = tgt_poly[k * XY : (k + 1) * XY, :].rearrange("r j -> (r j)")
-            queue.dma_start(tgt[:, k, :], rows.partition_broadcast(P))
+
+        def load_rows(first, count, queue):
+            rows = tgt_poly[first : first + count, :].rearrange("r j -> (r j)")
+            queue.dma_start(
+                tgt[:].rearrange("p k c -> p (k c)")[:, first * N : (first + count) * N],
+                rows.partition_broadcast(P),
+            )
+
+        for d in range(XY):
+            load_rows(0 * XY + d, 1, nc.sync)
+            load_rows(3 * XY + d, 1, nc.scalar)
+        load_rows(2 * XY, XY, nc.scalar)
+        scores = held.tile([P, BLOCKS, S], F32, name="scores")
+        nc.sync.dma_start(scores[:], logits.rearrange("(p b) s -> p b s", b=BLOCKS))
+        load_rows(1 * XY, XY, nc.sync)
+
+        offsets = held.tile([P, N // 16], U16, name="offsets")
+        nc.sync.dma_start(offsets[:], offs)
 
         def tgt_row(k, d):
             return tgt[:, k, d * N : (d + 1) * N]
 
+        def block(tile, b):
+            return tile[:, b * N : (b + 1) * N]
+
         ident = held.tile([P, P], F32, name="ident")
         make_identity(nc, ident[:])
-        pick = held.tile([P, STATS, P], F32, name="pick")
-        nc.vector.tensor_copy(pick[:], ident[:, 0:STATS].unsqueeze(2).to_broadcast([P, STATS, P]))
-        minus_half = held.tile([P, P], F32, name="minus_half")
-        nc.gpsimd.memset(minus_half[:], -0.5)
-        stat_rows = held.tile([P, XY * N], F32, name="stat_rows")
-        nc.gpsimd.memset(stat_rows[:], 0.0)
-
-        by_coord = pred[:].rearrange("p b k d -> p b d k")
-        a_hi = held.tile([P, BLOCKS, XY], F32, name="a_hi")
-        a_lo = held.tile([P, BLOCKS, XY], F32, name="a_lo")
-        nc.vector.tensor_reduce(out=a_hi[:], in_=by_coord, axis=X, op=ALU.max)
-        nc.vector.tensor_reduce(out=a_lo[:], in_=by_coord, axis=X, op=ALU.min)
-        a_side = held.tile([P, BLOCKS, XY], F32, name="a_side")
-        nc.vector.tensor_sub(a_side[:], a_hi[:], a_lo[:])
-        area1 = held.tile([P, BLOCKS], F32, name="area1")
-        nc.vector.tensor_mul(area1[:], a_side[:, :, 0], a_side[:, :, 1])
-        pred_sum = held.tile([P, BLOCKS], F32, name="pred_sum")
-        nc.vector.tensor_reduce(
-            out=pred_sum[:], in_=pred[:].rearrange("p b k d -> p b (k d)"), axis=X, op=ALU.add
-        )
-        pred_term = held.tile([P, BLOCKS], F32, name="pred_term")
-        nc.vector.tensor_scalar_mul(pred_term[:], pred_sum[:], -0.625)
-
-        neg_prob = []
-        for b in range(BLOCKS):
-            neg_max = held.tile([P, 1], F32, name=f"neg_max{b}")
-            nc.vector.tensor_reduce(out=neg_max[:], in_=scores[b][:], axis=X, op=ALU.max, negate=True)
-            expd = held.tile([P, S], F32, name=f"expd{b}")
-            total = held.tile([P, 1], F32, name=f"total{b}")
-            nc.scalar.activation(
-                out=expd[:], in_=scores[b][:], func=FN.Exp, bias=neg_max[:], scale=1.0, accum_out=total[:]
-            )
-            neg_total = held.tile([P, 1], F32, name=f"neg_total{b}")
-            nc.vector.tensor_scalar_mul(neg_total[:], total[:], -1.0)
-            neg_inv = held.tile([P, 1], F32, name=f"neg_inv{b}")
-            nc.vector.reciprocal(neg_inv[:], neg_total[:])
-            window = held.tile([P, S], F32, name=f"neg_prob{b}")
-            nc.scalar.activation(out=window[:], in_=expd[:], func=FN.Copy, scale=neg_inv[:])
-            neg_prob.append(window)
+        minus_half = held.tile([K * XY, P], F32, name="minus_half")
+        nc.vector.memset(minus_half[:], -0.5)
+        dummy = held.tile([P, 1], F32, name="dummy")
+        nc.vector.memset(dummy[:], 0.0)
+        warmed = held.tile([P, 1], F32, name="warmed")
+        nc.scalar.activation(out=warmed[:], in_=dummy[:], func=FN.Exp)
+        one = held.tile([P, 1], F32, name="one")
+        nc.vector.memset(one[:], 1.0)
 
         tgt_term = psum.tile([P, N], F32, name="tgt_term")
         nc.tensor.matmul(tgt_term[:], minus_half[:], tgt_rows[:], start=True, stop=True)
-
-        tgt_t = psum.tile([P, HALVES, P], F32, name="tgt_t")
+        tgt_t = psum.tile([P, HALVES, K * XY], F32, name="tgt_t")
         for h in range(HALVES):
-            nc.tensor.transpose(tgt_t[:, h, :], tgt_rows[:, h * P : (h + 1) * P], ident[:])
-        points_last = tgt_t[:, :, 0 : K * XY].rearrange("p h (k d) -> p d h k", d=XY)
-        stat = held.tile([P, XY, HALVES, STATS], F32, name="stat")
-        nc.vector.tensor_reduce(out=stat[:, :, :, LO], in_=points_last, axis=X, op=ALU.min)
-        nc.vector.tensor_reduce(out=stat[:, :, :, HI], in_=points_last, axis=X, op=ALU.max)
-        nc.vector.tensor_sub(stat[:, :, :, SIDE], stat[:, :, :, HI], stat[:, :, :, LO])
-        nc.vector.tensor_mul(
-            stat[:, :, :, AREA],
-            stat[:, 0:1, :, SIDE].to_broadcast([P, XY, HALVES]),
-            stat[:, 1:2, :, SIDE].to_broadcast([P, XY, HALVES]),
+            nc.tensor.matmul(
+                tgt_t[:, h, :], tgt_rows[:, h * P : (h + 1) * P], ident[0 : K * XY, 0 : K * XY],
+                start=True, stop=True,
+            )
+
+        neg_pred = held.tile([P, BLOCKS, K, XY], F32, name="neg_pred")
+        neg_max = held.tile([P, BLOCKS], F32, name="neg_max")
+        a_hi = held.tile([P, BLOCKS, XY], F32, name="a_hi")
+        a_lo = held.tile([P, BLOCKS, XY], F32, name="a_lo")
+        a_side = held.tile([P, BLOCKS, XY], F32, name="a_side")
+        area1 = held.tile([P, BLOCKS], F32, name="area1")
+        pred_sum = held.tile([P, BLOCKS], F32, name="pred_sum")
+        pred_term = held.tile([P, BLOCKS], F32, name="pred_term")
+        offloaded_sum = held.tile([P, BLOCKS], F32, name="offloaded_sum")
+        stat = held.tile([P, STATS, XY, HALVES], F32, name="stat")
+        pred_points_last = pred[:].rearrange("p b k d -> p b d k")
+        tgt_points_last = tgt_t[:].rearrange("p h (k d) -> p d h k", d=XY)
+
+        nc.vector.tensor_scalar_mul(neg_pred[:], pred[:], -1.0)
+        nc.vector.tensor_reduce(out=a_hi[:], in_=pred_points_last, axis=X, op=ALU.max)
+        nc.vector.tensor_reduce(out=a_lo[:], in_=pred_points_last, axis=X, op=ALU.min)
+        nc.vector.tensor_reduce(out=stat[:, HI, :, :], in_=tgt_points_last, axis=X, op=ALU.max)
+        nc.vector.tensor_reduce(out=stat[:, LO, :, :], in_=tgt_points_last, axis=X, op=ALU.min)
+        nc.vector.tensor_reduce(
+            out=pred_sum[:], in_=pred[:].rearrange("p b k d -> p b (k d)"), axis=X, op=ALU.add
         )
-        stat_t = psum.tile([P, XY * N], F32, name="stat_t")
-        for d in range(XY):
-            for h in range(HALVES):
-                first = d * N + h * P
-                nc.tensor.transpose(stat_t[0:STATS, first : first + P], stat[:, d, h, :], ident[:])
-        nc.scalar.copy(stat_rows[0:STATS, :], stat_t[0:STATS, :])
-        b_hi = psum.tile([P, XY * N], F32, name="b_hi")
-        b_lo = psum.tile([P, XY * N], F32, name="b_lo")
-        b_side = psum.tile([P, XY * N], F32, name="b_side")
-        area2 = psum.tile([P, N], F32, name="area2")
-        nc.tensor.matmul(b_hi[:], pick[:, HI, :], stat_rows[:], start=True, stop=True)
-        nc.tensor.matmul(b_lo[:], pick[:, LO, :], stat_rows[:], start=True, stop=True)
-        nc.tensor.matmul(b_side[:], pick[:, SIDE, :], stat_rows[:], start=True, stop=True)
-        nc.tensor.matmul(area2[:], pick[:, AREA, :], stat_rows[:, 0:N], start=True, stop=True)
+        nc.vector.tensor_reduce(
+            out=offloaded_sum[:], in_=pred[:, :, 0:OFFLOADED, :].rearrange("p b k d -> p b (k d)"),
+            axis=X, op=ALU.add,
+        )
+        nc.vector.tensor_sub(stat[:, SIDE, :, :], stat[:, HI, :, :], stat[:, LO, :, :])
+        nc.vector.tensor_sub(a_side[:], a_hi[:], a_lo[:])
+        nc.vector.tensor_scalar_mul(pred_term[:], pred_sum[:], -0.625)
+        nc.vector.tensor_mul(
+            stat[:, AREA, :, :],
+            stat[:, SIDE, 0:1, :].to_broadcast([P, XY, HALVES]),
+            stat[:, SIDE, 1:2, :].to_broadcast([P, XY, HALVES]),
+        )
+        nc.vector.tensor_mul(area1[:], a_side[:, :, 0], a_side[:, :, 1])
 
-        sums = [[tgt_term, tgt_term] for b in range(BLOCKS)]
+        def spread(s, coords, name):
+            row = psum.tile([P, coords * N], F32, name=name)
+            for d in range(coords):
+                for h in range(HALVES):
+                    first = d * N + h * P
+                    nc.tensor.transpose(
+                        row[:, first : first + P], stat[:, s, d, h : h + 1].to_broadcast([P, P]), ident[:]
+                    )
+            return row
 
-        def add_point(k):
+        b_hi = spread(HI, XY, "b_hi")
+        b_lo = spread(LO, XY, "b_lo")
+        b_side = spread(SIDE, XY, "b_side")
+        area2 = spread(AREA, 1, "area2")
+
+        offloaded_terms = psum.tile([P, BLOCKS * N], F32, name="offloaded_terms")
+
+        def make_terms(k):
+            terms = held.tile([P, XY, BLOCKS * N], F32, name=f"terms{k}")
             for d in range(XY):
                 for b in range(BLOCKS):
-                    for order, partner in enumerate((k, K - 1 - k)):
-                        longer = held.tile([P, N], F32, name=f"sum{b}{order}{k}{d}")
-                        nc.vector.scalar_tensor_tensor(
-                            out=longer[:],
-                            in0=tgt_row(partner, d),
-                            scalar=pred[:, b, k, d : d + 1],
-                            in1=sums[b][order][:],
-                            op0=ALU.max,
-                            op1=ALU.add,
-                        )
-                        sums[b][order] = longer
+                    nc.scalar.activation(
+                        out=block(terms[:, d, :], b), in_=tgt_row(K - 1 - k, d), func=FN.Relu,
+                        bias=neg_pred[:, b, k, d : d + 1], scale=1.0,
+                    )
+            return terms
 
-        add_point(0)
-        add_point(3)
-
-        tops = []
-        inverses = []
-        for b in range(BLOCKS):
-            overlap = held.tile([P, XY * N], F32, name=f"overlap{b}")
-            extent = held.tile([P, XY * N], F32, name=f"extent{b}")
+        def add_terms(k, terms):
             for d in range(XY):
-                cols = slice(d * N, (d + 1) * N)
-                hi, lo = a_hi[:, b, d : d + 1], a_lo[:, b, d : d + 1]
-                above = held.tile([P, N], F32, name=f"above{b}{d}")
-                nc.scalar.activation(out=above[:], in_=b_hi[:, cols], func=FN.Relu, bias=hi, scale=-1.0)
-                lost = held.tile([P, N], F32, name=f"lost{b}{d}")
-                nc.vector.scalar_tensor_tensor(
-                    out=lost[:], in0=b_lo[:, cols], scalar=lo, in1=above[:], op0=ALU.max, op1=ALU.add
+                nc.tensor.matmul(
+                    offloaded_terms[:], ident[:], terms[:, d, :],
+                    start=(k == 0 and d == 0), stop=(k == OFFLOADED - 1 and d == XY - 1),
                 )
-                nc.scalar.activation(out=overlap[:, cols], in_=lost[:], func=FN.Relu, bias=hi, scale=-1.0)
-                nc.vector.scalar_tensor_tensor(
-                    out=extent[:, cols], in0=lost[:], scalar=lo, in1=b_side[:, cols],
-                    op0=ALU.subtract, op1=ALU.add,
-                )
-            top = held.tile([P, 2 * N], F32, name=f"top{b}")
-            bottom = held.tile([P, 2 * N], F32, name=f"bottom{b}")
-            inter, union, hull = top[:, 0:N], bottom[:, 0:N], bottom[:, N : 2 * N]
-            nc.vector.tensor_mul(inter, overlap[:, 0:N], overlap[:, N : 2 * N])
-            nc.vector.tensor_mul(hull, extent[:, 0:N], extent[:, N : 2 * N])
-            nc.vector.scalar_tensor_tensor(
-                out=union, in0=area2[:], scalar=area1[:, b : b + 1], in1=inter, op0=ALU.add, op1=ALU.subtract
-            )
-            nc.vector.tensor_sub(top[:, N : 2 * N], hull, union)
-            floored = held.tile([P, 2 * N], F32, name=f"floored{b}")
-            nc.vector.tensor_scalar_max(floored[:], bottom[:], EPS)
-            logd = held.tile([P, 2 * N], F32, name=f"logd{b}")
-            nc.scalar.activation(out=logd[:], in_=floored[:], func=FN.Ln)
-            inverse = held.tile([P, 2 * N], F32, name=f"inverse{b}")
-            nc.scalar.activation(out=inverse[:], in_=logd[:], func=FN.Exp, scale=-1.0)
-            tops.append(top)
-            inverses.append(inverse)
 
-        add_point(1)
-        add_point(2)
+        def add_point(sums, k, partner, label):
+            for d in range(XY):
+                for b in range(BLOCKS):
+                    longer = held.tile([P, N], F32, name=f"{label}{b}{k}{d}")
+                    nc.vector.scalar_tensor_tensor(
+                        out=longer[:], in0=tgt_row(partner, d), scalar=pred[:, b, k, d : d + 1],
+                        in1=sums[b], op0=ALU.max, op1=ALU.add,
+                    )
+                    sums[b] = longer[:]
 
+        given_sum = [tgt_term[:] for b in range(BLOCKS)]
+        reversed_sum = [tgt_term[:] for b in range(BLOCKS)]
+        add_terms(0, make_terms(0))
+        add_terms(1, make_terms(1))
+        add_point(given_sum, 0, 0, "given")
+        add_point(given_sum, 3, 3, "given")
+        for k in range(OFFLOADED, K):
+            add_point(reversed_sum, k, K - 1 - k, "reversed")
+
+        expd = held.tile([P, BLOCKS, S], F32, name="expd")
+        total = held.tile([P, BLOCKS], F32, name="total")
+        nc.vector.tensor_reduce(out=neg_max[:], in_=scores[:], axis=X, op=ALU.max, negate=True)
         for b in range(BLOCKS):
-            best = held.tile([P, N], F32, name=f"best{b}")
-            nc.vector.tensor_tensor(best[:], sums[b][0][:], sums[b][1][:], ALU.min)
-            ratios = held.tile([P, 2 * N], F32, name=f"ratios{b}")
-            nc.vector.tensor_mul(ratios[:], tops[b][:], inverses[b][:])
-            partial = held.tile([P, N], F32, name=f"partial{b}")
-            nc.vector.scalar_tensor_tensor(
-                out=partial[:], in0=best[:], scalar=1.25, in1=ratios[:, 0:N], op0=ALU.mult, op1=ALU.subtract
+            nc.scalar.activation(
+                out=expd[:, b, :], in_=scores[:, b, :], func=FN.Exp, bias=neg_max[:, b : b + 1], scale=1.0,
+                accum_out=total[:, b : b + 1],
             )
-            others = held.tile([P, N], F32, name=f"others{b}")
+        nc.scalar.activation(out=warmed[:], in_=one[:], func=FN.Abs_reciprocal_sqrt)
+        add_terms(2, make_terms(2))
+
+        inner_hi = held.tile([P, BLOCKS, XY * N], F32, name="inner_hi")
+        neg_reach = held.tile([P, BLOCKS, XY * N], F32, name="neg_reach")
+        extent = held.tile([P, BLOCKS, XY * N], F32, name="extent")
+        neg_ov_y = held.tile([P, BLOCKS, N], F32, name="neg_ov_y")
+        top = held.tile([P, BLOCKS, 2 * N], F32, name="top")
+        bottom = held.tile([P, BLOCKS, 2 * N], F32, name="bottom")
+        floored = held.tile([P, BLOCKS, 2 * N], F32, name="floored")
+        root = held.tile([P, BLOCKS, 2 * N], F32, name="root")
+        inverse = held.tile([P, BLOCKS, 2 * N], F32, name="inverse")
+        first_half, second_half = slice(0, N), slice(N, 2 * N)
+        sides = [(b, d, slice(d * N, (d + 1) * N)) for b in range(BLOCKS) for d in range(XY)]
+
+        for b, d, cols in sides:
+            nc.vector.tensor_scalar_min(inner_hi[:, b, cols], b_hi[:, cols], a_hi[:, b, d : d + 1])
+        for b, d, cols in sides:
             nc.vector.scalar_tensor_tensor(
-                out=others[:], in0=partial[:], scalar=pred_term[:, b : b + 1], in1=ratios[:, N : 2 * N],
-                op0=ALU.add, op1=ALU.add,
+                out=neg_reach[:, b, cols], in0=b_lo[:, cols], scalar=a_lo[:, b, d : d + 1],
+                in1=inner_hi[:, b, cols], op0=ALU.max, op1=ALU.subtract,
             )
-            cost = held.tile([P, N], F32, name=f"cost{b}")
-            nc.vector.tensor_tensor(cost[:], neg_prob[b][:].indirect(offsets[:]), others[:], ALU.add)
-            nc.sync.dma_start(out[b * P : (b + 1) * P, :], cost[:])
+        for b, d, cols in sides:
+            nc.vector.scalar_tensor_tensor(
+                out=extent[:, b, cols], in0=b_side[:, cols], scalar=a_side[:, b, d : d + 1],
+                in1=neg_reach[:, b, cols], op0=ALU.add, op1=ALU.add,
+            )
+        for b in range(BLOCKS):
+            nc.vector.tensor_scalar_min(neg_ov_y[:, b, :], neg_reach[:, b, second_half], 0.0)
+        for b in range(BLOCKS):
+            nc.vector.tensor_mul(bottom[:, b, second_half], extent[:, b, first_half], extent[:, b, second_half])
+        for b in range(BLOCKS):
+            nc.vector.scalar_tensor_tensor(
+                out=top[:, b, first_half], in0=neg_reach[:, b, first_half], scalar=0.0, in1=neg_ov_y[:, b, :],
+                op0=ALU.min, op1=ALU.mult,
+            )
+        for b in range(BLOCKS):
+            nc.vector.scalar_tensor_tensor(
+                out=bottom[:, b, first_half], in0=area2[:], scalar=area1[:, b : b + 1],
+                in1=top[:, b, first_half], op0=ALU.add, op1=ALU.subtract,
+            )
+        for b in range(BLOCKS):
+            nc.vector.tensor_sub(top[:, b, second_half], bottom[:, b, second_half], bottom[:, b, first_half])
+        for b in range(BLOCKS):
+            nc.vector.tensor_scalar_max(floored[:, b, :], bottom[:, b, :], EPS)
+        for b in range(BLOCKS):
+            nc.scalar.activation(out=root[:, b, :], in_=floored[:, b, :], func=FN.Abs_reciprocal_sqrt)
+        for b in range(BLOCKS):
+            nc.scalar.activation(out=inverse[:, b, :], in_=root[:, b, :], func=FN.Square)
+
+        neg_total = held.tile([P, BLOCKS], F32, name="neg_total")
+        neg_inv = held.tile([P, BLOCKS], F32, name="neg_inv")
+        neg_prob = [held.tile([P, S], F32, name=f"neg_prob{b}") for b in range(BLOCKS)]
+        nc.vector.tensor_scalar_mul(neg_total[:], total[:], -1.0)
+        add_point(given_sum, 2, 2, "given")
+        nc.vector.reciprocal(neg_inv[:], neg_total[:])
+        add_point(given_sum, 1, 1, "given")
+        for b in range(BLOCKS):
+            nc.scalar.activation(out=neg_prob[b][:], in_=expd[:, b, :], func=FN.Copy, scale=neg_inv[:, b : b + 1])
+
+        ratios = held.tile([P, BLOCKS, 2 * N], F32, name="ratios")
+        rest = held.tile([P, BLOCKS, N], F32, name="rest")
+        whole_reversed = held.tile([P, BLOCKS, N], F32, name="whole_reversed")
+        best = held.tile([P, BLOCKS, N], F32, name="best")
+        others = held.tile([P, BLOCKS, N], F32, name="others")
+        cost = [held.tile([P, N], F32, name=f"cost{b}") for b in range(BLOCKS)]
+        for b in range(BLOCKS):
+            nc.vector.tensor_mul(ratios[:, b, :], top[:, b, :], inverse[:, b, :])
+        for b in range(BLOCKS):
+            nc.vector.scalar_tensor_tensor(
+                out=whole_reversed[:, b, :], in0=block(offloaded_terms, b), scalar=offloaded_sum[:, b : b + 1],
+                in1=reversed_sum[b], op0=ALU.add, op1=ALU.add,
+            )
+        for b in range(BLOCKS):
+            nc.vector.scalar_tensor_tensor(
+                out=rest[:, b, :], in0=ratios[:, b, second_half], scalar=pred_term[:, b : b + 1],
+                in1=ratios[:, b, first_half], op0=ALU.add, op1=ALU.subtract,
+            )
+        for b in range(BLOCKS):
+            nc.vector.tensor_tensor(best[:, b, :], whole_reversed[:, b, :], given_sum[b], ALU.min)
+        for b in range(BLOCKS):
+            nc.vector.scalar_tensor_tensor(
+                out=others[:, b, :], in0=best[:, b, :], scalar=1.25, in1=rest[:, b, :],
+                op0=ALU.mult, op1=ALU.add,
+            )
+        for b, queue in enumerate((nc.sync, nc.scalar)):
+            nc.vector.tensor_tensor(cost[b][:], neg_prob[b][:].indirect(offsets[:]), others[:, b, :], ALU.add)
+            queue.dma_start(out.rearrange("(p b) j -> p b j", b=BLOCKS)[:, b, :], cost[b][:])

@@ -10,18 +10,17 @@ X = mybir.AxisListType.X
 P = 128
 Q, S, N = 256, 256, 256
 K, XY = 4, 2
+ROWS = K * XY
 BLOCKS = Q // P
 HALVES = N // P
 EPS = 1e-6
-LO, HI, SIDE, AREA = 0, 1, 2, 3
-STATS = 4
 OFFLOADED = 3
 
 
 def tile_hungarianmatcherpolyline_kernel(tc, logits, pred_poly, tgt_poly, offs, out):
     nc = tc.nc
     with tc.tile_pool(name="held", bufs=1) as held, tc.psum_pool(name="psum", bufs=1) as psum:
-        tgt_rows = held.tile([K * XY, N], F32, name="tgt_rows")
+        tgt_rows = held.tile([ROWS, N], F32, name="tgt_rows")
         nc.scalar.dma_start(tgt_rows[:], tgt_poly)
 
         pred = held.tile([P, BLOCKS, K, XY], F32, name="pred")
@@ -55,26 +54,25 @@ def tile_hungarianmatcherpolyline_kernel(tc, logits, pred_poly, tgt_poly, offs, 
 
         ident = held.tile([P, P], F32, name="ident")
         make_identity(nc, ident[:])
-        minus_half = held.tile([K * XY, P], F32, name="minus_half")
-        nc.vector.memset(minus_half[:], -0.5)
         dummy = held.tile([P, 1], F32, name="dummy")
         nc.vector.memset(dummy[:], 0.0)
         warmed = held.tile([P, 1], F32, name="warmed")
         nc.scalar.activation(out=warmed[:], in_=dummy[:], func=FN.Exp)
-        one = held.tile([P, 1], F32, name="one")
-        nc.vector.memset(one[:], 1.0)
 
-        tgt_term = psum.tile([P, N], F32, name="tgt_term")
-        nc.tensor.matmul(tgt_term[:], minus_half[:], tgt_rows[:], start=True, stop=True)
-        tgt_t = psum.tile([P, HALVES, K * XY], F32, name="tgt_t")
+        tgt_t = psum.tile([P, HALVES, ROWS], F32, name="tgt_t")
         for h in range(HALVES):
             nc.tensor.matmul(
-                tgt_t[:, h, :], tgt_rows[:, h * P : (h + 1) * P], ident[0 : K * XY, 0 : K * XY],
-                start=True, stop=True,
+                tgt_t[:, h, :], tgt_rows[:, h * P : (h + 1) * P], ident[0:ROWS, 0:ROWS], start=True, stop=True
             )
+        tgt_points_last = tgt_t[:].rearrange("p h (k d) -> p d h k", d=XY)
+        pred_points_last = pred[:].rearrange("p b k d -> p b d k")
 
+        col_hi = held.tile([P, XY, HALVES], F32, name="col_hi")
+        col_lo = held.tile([P, XY, HALVES], F32, name="col_lo")
+        col_side = held.tile([P, XY, HALVES], F32, name="col_side")
+        col_area = held.tile([P, 1, HALVES], F32, name="col_area")
+        col_sum = held.tile([P, 1, HALVES], F32, name="col_sum")
         neg_pred = held.tile([P, BLOCKS, K, XY], F32, name="neg_pred")
-        neg_max = held.tile([P, BLOCKS], F32, name="neg_max")
         a_hi = held.tile([P, BLOCKS, XY], F32, name="a_hi")
         a_lo = held.tile([P, BLOCKS, XY], F32, name="a_lo")
         a_side = held.tile([P, BLOCKS, XY], F32, name="a_side")
@@ -82,50 +80,45 @@ def tile_hungarianmatcherpolyline_kernel(tc, logits, pred_poly, tgt_poly, offs, 
         pred_sum = held.tile([P, BLOCKS], F32, name="pred_sum")
         pred_term = held.tile([P, BLOCKS], F32, name="pred_term")
         offloaded_sum = held.tile([P, BLOCKS], F32, name="offloaded_sum")
-        stat = held.tile([P, STATS, XY, HALVES], F32, name="stat")
-        pred_points_last = pred[:].rearrange("p b k d -> p b d k")
-        tgt_points_last = tgt_t[:].rearrange("p h (k d) -> p d h k", d=XY)
 
+        nc.vector.tensor_reduce(out=col_hi[:], in_=tgt_points_last, axis=X, op=ALU.max)
+        nc.vector.tensor_reduce(out=col_lo[:], in_=tgt_points_last, axis=X, op=ALU.min)
         nc.vector.tensor_scalar_mul(neg_pred[:], pred[:], -1.0)
         nc.vector.tensor_reduce(out=a_hi[:], in_=pred_points_last, axis=X, op=ALU.max)
         nc.vector.tensor_reduce(out=a_lo[:], in_=pred_points_last, axis=X, op=ALU.min)
-        nc.vector.tensor_reduce(out=stat[:, HI, :, :], in_=tgt_points_last, axis=X, op=ALU.max)
-        nc.vector.tensor_reduce(out=stat[:, LO, :, :], in_=tgt_points_last, axis=X, op=ALU.min)
-        nc.vector.tensor_reduce(
-            out=pred_sum[:], in_=pred[:].rearrange("p b k d -> p b (k d)"), axis=X, op=ALU.add
-        )
+        nc.vector.tensor_sub(col_side[:], col_hi[:], col_lo[:])
+        nc.vector.tensor_reduce(out=col_sum[:, 0, :], in_=tgt_t[:], axis=X, op=ALU.add)
+        nc.vector.tensor_sub(a_side[:], a_hi[:], a_lo[:])
+        nc.vector.tensor_mul(col_area[:, 0, :], col_side[:, 0, :], col_side[:, 1, :])
+        nc.vector.tensor_mul(area1[:], a_side[:, :, 0], a_side[:, :, 1])
         nc.vector.tensor_reduce(
             out=offloaded_sum[:], in_=pred[:, :, 0:OFFLOADED, :].rearrange("p b k d -> p b (k d)"),
             axis=X, op=ALU.add,
         )
-        nc.vector.tensor_sub(stat[:, SIDE, :, :], stat[:, HI, :, :], stat[:, LO, :, :])
-        nc.vector.tensor_sub(a_side[:], a_hi[:], a_lo[:])
-        nc.vector.tensor_scalar_mul(pred_term[:], pred_sum[:], -0.625)
-        nc.vector.tensor_mul(
-            stat[:, AREA, :, :],
-            stat[:, SIDE, 0:1, :].to_broadcast([P, XY, HALVES]),
-            stat[:, SIDE, 1:2, :].to_broadcast([P, XY, HALVES]),
+        nc.vector.tensor_reduce(
+            out=pred_sum[:], in_=pred[:].rearrange("p b k d -> p b (k d)"), axis=X, op=ALU.add
         )
-        nc.vector.tensor_mul(area1[:], a_side[:, :, 0], a_side[:, :, 1])
+        nc.vector.tensor_scalar_mul(pred_term[:], pred_sum[:], -0.625)
 
-        def spread(s, coords, name):
+        def spread(columns, coords, name):
             row = psum.tile([P, coords * N], F32, name=name)
             for d in range(coords):
                 for h in range(HALVES):
                     first = d * N + h * P
                     nc.tensor.transpose(
-                        row[:, first : first + P], stat[:, s, d, h : h + 1].to_broadcast([P, P]), ident[:]
+                        row[:, first : first + P], columns[:, d, h : h + 1].to_broadcast([P, P]), ident[:]
                     )
             return row
 
-        b_hi = spread(HI, XY, "b_hi")
-        b_lo = spread(LO, XY, "b_lo")
-        b_side = spread(SIDE, XY, "b_side")
-        area2 = spread(AREA, 1, "area2")
+        b_hi = spread(col_hi, XY, "b_hi")
+        b_lo = spread(col_lo, XY, "b_lo")
+        b_side = spread(col_side, XY, "b_side")
+        area2 = spread(col_area, 1, "area2")
+        tgt_sum = spread(col_sum, 1, "tgt_sum")
 
         offloaded_terms = psum.tile([P, BLOCKS * N], F32, name="offloaded_terms")
 
-        def make_terms(k):
+        def offload_point(k):
             terms = held.tile([P, XY, BLOCKS * N], F32, name=f"terms{k}")
             for d in range(XY):
                 for b in range(BLOCKS):
@@ -133,127 +126,151 @@ def tile_hungarianmatcherpolyline_kernel(tc, logits, pred_poly, tgt_poly, offs, 
                         out=block(terms[:, d, :], b), in_=tgt_row(K - 1 - k, d), func=FN.Relu,
                         bias=neg_pred[:, b, k, d : d + 1], scale=1.0,
                     )
-            return terms
-
-        def add_terms(k, terms):
-            for d in range(XY):
                 nc.tensor.matmul(
                     offloaded_terms[:], ident[:], terms[:, d, :],
                     start=(k == 0 and d == 0), stop=(k == OFFLOADED - 1 and d == XY - 1),
                 )
 
-        def add_point(sums, k, partner, label):
-            for d in range(XY):
-                for b in range(BLOCKS):
-                    longer = held.tile([P, N], F32, name=f"{label}{b}{k}{d}")
+        def add_terms(sums, label, k, partner, d):
+            for b in range(BLOCKS):
+                longer = held.tile([P, N], F32, name=f"{label}{b}{k}{d}")
+                if sums[b] is None:
+                    nc.vector.tensor_scalar_max(longer[:], tgt_row(partner, d), pred[:, b, k, d : d + 1])
+                else:
                     nc.vector.scalar_tensor_tensor(
                         out=longer[:], in0=tgt_row(partner, d), scalar=pred[:, b, k, d : d + 1],
                         in1=sums[b], op0=ALU.max, op1=ALU.add,
                     )
-                    sums[b] = longer[:]
+                sums[b] = longer[:]
 
-        given_sum = [tgt_term[:] for b in range(BLOCKS)]
-        reversed_sum = [tgt_term[:] for b in range(BLOCKS)]
-        add_terms(0, make_terms(0))
-        add_terms(1, make_terms(1))
-        add_point(given_sum, 0, 0, "given")
-        add_point(given_sum, 3, 3, "given")
-        for k in range(OFFLOADED, K):
-            add_point(reversed_sum, k, K - 1 - k, "reversed")
+        given_sum = [None for b in range(BLOCKS)]
+        left_sum = [None for b in range(BLOCKS)]
 
+        offload_point(0)
+        for d in range(XY):
+            add_terms(given_sum, "given", 0, 0, d)
+            for k in range(OFFLOADED, K):
+                add_terms(left_sum, "left", k, K - 1 - k, d)
+
+        neg_max = held.tile([P, BLOCKS], F32, name="neg_max")
         expd = held.tile([P, BLOCKS, S], F32, name="expd")
         total = held.tile([P, BLOCKS], F32, name="total")
         nc.vector.tensor_reduce(out=neg_max[:], in_=scores[:], axis=X, op=ALU.max, negate=True)
+
+        above = held.tile([P, BLOCKS, XY * N], F32, name="above")
+        lost = held.tile([P, BLOCKS, XY * N], F32, name="lost")
+        overlap = held.tile([P, BLOCKS, XY * N], F32, name="overlap")
+        extent = held.tile([P, BLOCKS, XY * N], F32, name="extent")
+        x_cols, y_cols = slice(0, N), slice(N, XY * N)
+        sides = [(b, d, slice(d * N, (d + 1) * N)) for b in range(BLOCKS) for d in range(XY)]
+
+        def per_block(name):
+            return held.tile([P, BLOCKS, N], F32, name=name)
+
+        for b, d, cols in sides:
+            nc.scalar.activation(
+                out=above[:, b, cols], in_=b_hi[:, cols], func=FN.Relu, bias=a_hi[:, b, d : d + 1], scale=-1.0
+            )
         for b in range(BLOCKS):
             nc.scalar.activation(
                 out=expd[:, b, :], in_=scores[:, b, :], func=FN.Exp, bias=neg_max[:, b : b + 1], scale=1.0,
                 accum_out=total[:, b : b + 1],
             )
-        nc.scalar.activation(out=warmed[:], in_=one[:], func=FN.Abs_reciprocal_sqrt)
-        add_terms(2, make_terms(2))
-
-        inner_hi = held.tile([P, BLOCKS, XY * N], F32, name="inner_hi")
-        neg_reach = held.tile([P, BLOCKS, XY * N], F32, name="neg_reach")
-        extent = held.tile([P, BLOCKS, XY * N], F32, name="extent")
-        neg_ov_y = held.tile([P, BLOCKS, N], F32, name="neg_ov_y")
-        top = held.tile([P, BLOCKS, 2 * N], F32, name="top")
-        bottom = held.tile([P, BLOCKS, 2 * N], F32, name="bottom")
-        floored = held.tile([P, BLOCKS, 2 * N], F32, name="floored")
-        root = held.tile([P, BLOCKS, 2 * N], F32, name="root")
-        inverse = held.tile([P, BLOCKS, 2 * N], F32, name="inverse")
-        first_half, second_half = slice(0, N), slice(N, 2 * N)
-        sides = [(b, d, slice(d * N, (d + 1) * N)) for b in range(BLOCKS) for d in range(XY)]
-
-        for b, d, cols in sides:
-            nc.vector.tensor_scalar_min(inner_hi[:, b, cols], b_hi[:, cols], a_hi[:, b, d : d + 1])
         for b, d, cols in sides:
             nc.vector.scalar_tensor_tensor(
-                out=neg_reach[:, b, cols], in0=b_lo[:, cols], scalar=a_lo[:, b, d : d + 1],
-                in1=inner_hi[:, b, cols], op0=ALU.max, op1=ALU.subtract,
+                out=lost[:, b, cols], in0=b_lo[:, cols], scalar=a_lo[:, b, d : d + 1],
+                in1=above[:, b, cols], op0=ALU.max, op1=ALU.add,
+            )
+        offload_point(1)
+        for d in range(XY):
+            add_terms(given_sum, "given", 3, 3, d)
+        for b, d, cols in sides:
+            nc.scalar.activation(
+                out=overlap[:, b, cols], in_=lost[:, b, cols], func=FN.Relu, bias=a_hi[:, b, d : d + 1], scale=-1.0
             )
         for b, d, cols in sides:
             nc.vector.scalar_tensor_tensor(
-                out=extent[:, b, cols], in0=b_side[:, cols], scalar=a_side[:, b, d : d + 1],
-                in1=neg_reach[:, b, cols], op0=ALU.add, op1=ALU.add,
+                out=extent[:, b, cols], in0=lost[:, b, cols], scalar=a_lo[:, b, d : d + 1],
+                in1=b_side[:, cols], op0=ALU.subtract, op1=ALU.add,
             )
+        offload_point(2)
+        hull, hull_floor, hull_root, hull_inv = (per_block(f"hull{s}") for s in ("", "_floor", "_root", "_inv"))
+        union, union_floor, union_root, union_inv = (per_block(f"union{s}") for s in ("", "_floor", "_root", "_inv"))
+        inter = per_block("inter")
+        excess = per_block("excess")
         for b in range(BLOCKS):
-            nc.vector.tensor_scalar_min(neg_ov_y[:, b, :], neg_reach[:, b, second_half], 0.0)
+            nc.vector.tensor_mul(hull[:, b, :], extent[:, b, x_cols], extent[:, b, y_cols])
         for b in range(BLOCKS):
-            nc.vector.tensor_mul(bottom[:, b, second_half], extent[:, b, first_half], extent[:, b, second_half])
+            nc.vector.tensor_scalar_max(hull_floor[:, b, :], hull[:, b, :], EPS)
+        add_terms(given_sum, "given", 2, 2, 0)
+        for b in range(BLOCKS):
+            nc.vector.tensor_mul(inter[:, b, :], overlap[:, b, x_cols], overlap[:, b, y_cols])
+        add_terms(given_sum, "given", 2, 2, 1)
         for b in range(BLOCKS):
             nc.vector.scalar_tensor_tensor(
-                out=top[:, b, first_half], in0=neg_reach[:, b, first_half], scalar=0.0, in1=neg_ov_y[:, b, :],
-                op0=ALU.min, op1=ALU.mult,
+                out=union[:, b, :], in0=area2[:], scalar=area1[:, b : b + 1], in1=inter[:, b, :],
+                op0=ALU.add, op1=ALU.subtract,
             )
-        for b in range(BLOCKS):
-            nc.vector.scalar_tensor_tensor(
-                out=bottom[:, b, first_half], in0=area2[:], scalar=area1[:, b : b + 1],
-                in1=top[:, b, first_half], op0=ALU.add, op1=ALU.subtract,
-            )
-        for b in range(BLOCKS):
-            nc.vector.tensor_sub(top[:, b, second_half], bottom[:, b, second_half], bottom[:, b, first_half])
-        for b in range(BLOCKS):
-            nc.vector.tensor_scalar_max(floored[:, b, :], bottom[:, b, :], EPS)
-        for b in range(BLOCKS):
-            nc.scalar.activation(out=root[:, b, :], in_=floored[:, b, :], func=FN.Abs_reciprocal_sqrt)
-        for b in range(BLOCKS):
-            nc.scalar.activation(out=inverse[:, b, :], in_=root[:, b, :], func=FN.Square)
 
-        neg_total = held.tile([P, BLOCKS], F32, name="neg_total")
-        neg_inv = held.tile([P, BLOCKS], F32, name="neg_inv")
+        tgt_term = held.tile([P, N], F32, name="tgt_term")
+        nc.scalar.activation(out=tgt_term[:], in_=tgt_sum[:], func=FN.Copy, scale=-0.625)
+        nc.scalar.activation(out=warmed[:], in_=total[:, BLOCKS - 1 : BLOCKS], func=FN.Abs_reciprocal_sqrt)
+
+        def invert(floor, root, inv):
+            for b in range(BLOCKS):
+                nc.scalar.activation(out=root[:, b, :], in_=floor[:, b, :], func=FN.Abs_reciprocal_sqrt)
+            for b in range(BLOCKS):
+                nc.scalar.activation(out=inv[:, b, :], in_=root[:, b, :], func=FN.Square)
+
+        invert(hull_floor, hull_root, hull_inv)
+        add_terms(given_sum, "given", 1, 1, 0)
+        for b in range(BLOCKS):
+            nc.vector.tensor_scalar_max(union_floor[:, b, :], union[:, b, :], EPS)
+        invert(union_floor, union_root, union_inv)
+        for b in range(BLOCKS):
+            nc.vector.tensor_sub(excess[:, b, :], hull[:, b, :], union[:, b, :])
+        add_terms(given_sum, "given", 1, 1, 1)
+
+        inv_total = held.tile([P, BLOCKS], F32, name="inv_total")
         neg_prob = [held.tile([P, S], F32, name=f"neg_prob{b}") for b in range(BLOCKS)]
-        nc.vector.tensor_scalar_mul(neg_total[:], total[:], -1.0)
-        add_point(given_sum, 2, 2, "given")
-        nc.vector.reciprocal(neg_inv[:], neg_total[:])
-        add_point(given_sum, 1, 1, "given")
+        picked = [held.tile([P, N], F32, name=f"picked{b}") for b in range(BLOCKS)]
+        nc.vector.reciprocal(inv_total[:], total[:])
         for b in range(BLOCKS):
-            nc.scalar.activation(out=neg_prob[b][:], in_=expd[:, b, :], func=FN.Copy, scale=neg_inv[:, b : b + 1])
+            nc.vector.tensor_scalar(
+                out=neg_prob[b][:], in0=expd[:, b, :], scalar1=inv_total[:, b : b + 1], scalar2=-1.0,
+                op0=ALU.mult, op1=ALU.mult,
+            )
+        for b in range(BLOCKS):
+            nc.vector.tensor_tensor(picked[b][:], neg_prob[b][:].indirect(offsets[:]), tgt_term[:], ALU.add)
 
-        ratios = held.tile([P, BLOCKS, 2 * N], F32, name="ratios")
-        rest = held.tile([P, BLOCKS, N], F32, name="rest")
-        whole_reversed = held.tile([P, BLOCKS, N], F32, name="whole_reversed")
-        best = held.tile([P, BLOCKS, N], F32, name="best")
-        others = held.tile([P, BLOCKS, N], F32, name="others")
+        reversed_sum = per_block("reversed_sum")
+        best = per_block("best")
+        with_poly = per_block("with_poly")
+        excess_ratio = per_block("excess_ratio")
+        inter_ratio = per_block("inter_ratio")
+        with_excess = per_block("with_excess")
         cost = [held.tile([P, N], F32, name=f"cost{b}") for b in range(BLOCKS)]
         for b in range(BLOCKS):
-            nc.vector.tensor_mul(ratios[:, b, :], top[:, b, :], inverse[:, b, :])
+            nc.vector.tensor_mul(excess_ratio[:, b, :], excess[:, b, :], hull_inv[:, b, :])
         for b in range(BLOCKS):
             nc.vector.scalar_tensor_tensor(
-                out=whole_reversed[:, b, :], in0=block(offloaded_terms, b), scalar=offloaded_sum[:, b : b + 1],
-                in1=reversed_sum[b], op0=ALU.add, op1=ALU.add,
+                out=reversed_sum[:, b, :], in0=block(offloaded_terms, b), scalar=offloaded_sum[:, b : b + 1],
+                in1=left_sum[b], op0=ALU.add, op1=ALU.add,
             )
         for b in range(BLOCKS):
-            nc.vector.scalar_tensor_tensor(
-                out=rest[:, b, :], in0=ratios[:, b, second_half], scalar=pred_term[:, b : b + 1],
-                in1=ratios[:, b, first_half], op0=ALU.add, op1=ALU.subtract,
-            )
-        for b in range(BLOCKS):
-            nc.vector.tensor_tensor(best[:, b, :], whole_reversed[:, b, :], given_sum[b], ALU.min)
+            nc.vector.tensor_tensor(best[:, b, :], reversed_sum[:, b, :], given_sum[b], ALU.min)
         for b in range(BLOCKS):
             nc.vector.scalar_tensor_tensor(
-                out=others[:, b, :], in0=best[:, b, :], scalar=1.25, in1=rest[:, b, :],
+                out=with_poly[:, b, :], in0=best[:, b, :], scalar=1.25, in1=picked[b][:],
                 op0=ALU.mult, op1=ALU.add,
             )
+        for b in range(BLOCKS):
+            nc.vector.scalar_tensor_tensor(
+                out=with_excess[:, b, :], in0=with_poly[:, b, :], scalar=pred_term[:, b : b + 1],
+                in1=excess_ratio[:, b, :], op0=ALU.add, op1=ALU.add,
+            )
+        for b in range(BLOCKS):
+            nc.vector.tensor_mul(inter_ratio[:, b, :], inter[:, b, :], union_inv[:, b, :])
         for b, queue in enumerate((nc.sync, nc.scalar)):
-            nc.vector.tensor_tensor(cost[b][:], neg_prob[b][:].indirect(offsets[:]), others[:, b, :], ALU.add)
+            nc.vector.tensor_sub(cost[b][:], with_excess[:, b, :], inter_ratio[:, b, :])
             queue.dma_start(out.rearrange("(p b) j -> p b j", b=BLOCKS)[:, b, :], cost[b][:])

@@ -14,7 +14,11 @@ ROWS = K * XY
 BLOCKS = Q // P
 HALVES = N // P
 EPS = 1e-6
-OFFLOADED = 3
+OFFLOADED = 5
+
+
+def reversed_partner(c):
+    return (K - 1 - c // XY) * XY + c % XY
 
 
 def tile_hungarianmatcherpolyline_kernel(tc, logits, pred_poly, tgt_poly, offs, out):
@@ -23,15 +27,15 @@ def tile_hungarianmatcherpolyline_kernel(tc, logits, pred_poly, tgt_poly, offs, 
         tgt_rows = held.tile([ROWS, N], F32, name="tgt_rows")
         nc.scalar.dma_start(tgt_rows[:], tgt_poly)
 
-        pred = held.tile([P, BLOCKS, K, XY], F32, name="pred")
-        nc.sync.dma_start(pred[:], pred_poly.rearrange("(p b) (k d) -> p b k d", b=BLOCKS, d=XY))
+        pred = held.tile([P, BLOCKS, ROWS], F32, name="pred")
+        nc.sync.dma_start(pred[:], pred_poly.rearrange("(p b) c -> p b c", b=BLOCKS))
 
-        tgt = held.tile([P, K, XY * N], F32, name="tgt")
+        tgt = held.tile([P, ROWS, N], F32, name="tgt")
 
         def load_rows(first, count, queue):
             rows = tgt_poly[first : first + count, :].rearrange("r j -> (r j)")
             queue.dma_start(
-                tgt[:].rearrange("p k c -> p (k c)")[:, first * N : (first + count) * N],
+                tgt[:].rearrange("p r j -> p (r j)")[:, first * N : (first + count) * N],
                 rows.partition_broadcast(P),
             )
 
@@ -45,9 +49,6 @@ def tile_hungarianmatcherpolyline_kernel(tc, logits, pred_poly, tgt_poly, offs, 
 
         offsets = held.tile([P, N // 16], U16, name="offsets")
         nc.sync.dma_start(offsets[:], offs)
-
-        def tgt_row(k, d):
-            return tgt[:, k, d * N : (d + 1) * N]
 
         def block(tile, b):
             return tile[:, b * N : (b + 1) * N]
@@ -65,14 +66,14 @@ def tile_hungarianmatcherpolyline_kernel(tc, logits, pred_poly, tgt_poly, offs, 
                 tgt_t[:, h, :], tgt_rows[:, h * P : (h + 1) * P], ident[0:ROWS, 0:ROWS], start=True, stop=True
             )
         tgt_points_last = tgt_t[:].rearrange("p h (k d) -> p d h k", d=XY)
-        pred_points_last = pred[:].rearrange("p b k d -> p b d k")
+        pred_points_last = pred[:].rearrange("p b (k d) -> p b d k", d=XY)
 
         col_hi = held.tile([P, XY, HALVES], F32, name="col_hi")
         col_lo = held.tile([P, XY, HALVES], F32, name="col_lo")
         col_side = held.tile([P, XY, HALVES], F32, name="col_side")
         col_area = held.tile([P, 1, HALVES], F32, name="col_area")
         col_sum = held.tile([P, 1, HALVES], F32, name="col_sum")
-        neg_pred = held.tile([P, BLOCKS, K, XY], F32, name="neg_pred")
+        neg_pred = held.tile([P, BLOCKS, ROWS], F32, name="neg_pred")
         a_hi = held.tile([P, BLOCKS, XY], F32, name="a_hi")
         a_lo = held.tile([P, BLOCKS, XY], F32, name="a_lo")
         a_side = held.tile([P, BLOCKS, XY], F32, name="a_side")
@@ -91,13 +92,8 @@ def tile_hungarianmatcherpolyline_kernel(tc, logits, pred_poly, tgt_poly, offs, 
         nc.vector.tensor_sub(a_side[:], a_hi[:], a_lo[:])
         nc.vector.tensor_mul(col_area[:, 0, :], col_side[:, 0, :], col_side[:, 1, :])
         nc.vector.tensor_mul(area1[:], a_side[:, :, 0], a_side[:, :, 1])
-        nc.vector.tensor_reduce(
-            out=offloaded_sum[:], in_=pred[:, :, 0:OFFLOADED, :].rearrange("p b k d -> p b (k d)"),
-            axis=X, op=ALU.add,
-        )
-        nc.vector.tensor_reduce(
-            out=pred_sum[:], in_=pred[:].rearrange("p b k d -> p b (k d)"), axis=X, op=ALU.add
-        )
+        nc.vector.tensor_reduce(out=offloaded_sum[:], in_=pred[:, :, 0:OFFLOADED], axis=X, op=ALU.add)
+        nc.vector.tensor_reduce(out=pred_sum[:], in_=pred[:], axis=X, op=ALU.add)
         nc.vector.tensor_scalar_mul(pred_term[:], pred_sum[:], -0.625)
 
         def spread(columns, coords, name):
@@ -118,27 +114,23 @@ def tile_hungarianmatcherpolyline_kernel(tc, logits, pred_poly, tgt_poly, offs, 
 
         offloaded_terms = psum.tile([P, BLOCKS * N], F32, name="offloaded_terms")
 
-        def offload_point(k):
-            terms = held.tile([P, XY, BLOCKS * N], F32, name=f"terms{k}")
-            for d in range(XY):
-                for b in range(BLOCKS):
-                    nc.scalar.activation(
-                        out=block(terms[:, d, :], b), in_=tgt_row(K - 1 - k, d), func=FN.Relu,
-                        bias=neg_pred[:, b, k, d : d + 1], scale=1.0,
-                    )
-                nc.tensor.matmul(
-                    offloaded_terms[:], ident[:], terms[:, d, :],
-                    start=(k == 0 and d == 0), stop=(k == OFFLOADED - 1 and d == XY - 1),
-                )
-
-        def add_terms(sums, label, k, partner, d):
+        def offload_term(c):
+            term = held.tile([P, BLOCKS * N], F32, name=f"term{c}")
             for b in range(BLOCKS):
-                longer = held.tile([P, N], F32, name=f"{label}{b}{k}{d}")
+                nc.scalar.activation(
+                    out=block(term, b), in_=tgt[:, reversed_partner(c), :], func=FN.Relu,
+                    bias=neg_pred[:, b, c : c + 1], scale=1.0,
+                )
+            nc.tensor.matmul(offloaded_terms[:], ident[:], term[:], start=(c == 0), stop=(c == OFFLOADED - 1))
+
+        def add_term(sums, label, c, row):
+            for b in range(BLOCKS):
+                longer = held.tile([P, N], F32, name=f"{label}{b}{c}")
                 if sums[b] is None:
-                    nc.vector.tensor_scalar_max(longer[:], tgt_row(partner, d), pred[:, b, k, d : d + 1])
+                    nc.vector.tensor_scalar_max(longer[:], tgt[:, row, :], pred[:, b, c : c + 1])
                 else:
                     nc.vector.scalar_tensor_tensor(
-                        out=longer[:], in0=tgt_row(partner, d), scalar=pred[:, b, k, d : d + 1],
+                        out=longer[:], in0=tgt[:, row, :], scalar=pred[:, b, c : c + 1],
                         in1=sums[b], op0=ALU.max, op1=ALU.add,
                     )
                 sums[b] = longer[:]
@@ -146,11 +138,15 @@ def tile_hungarianmatcherpolyline_kernel(tc, logits, pred_poly, tgt_poly, offs, 
         given_sum = [None for b in range(BLOCKS)]
         left_sum = [None for b in range(BLOCKS)]
 
-        offload_point(0)
-        for d in range(XY):
-            add_terms(given_sum, "given", 0, 0, d)
-            for k in range(OFFLOADED, K):
-                add_terms(left_sum, "left", k, K - 1 - k, d)
+        def use_row(row):
+            add_term(given_sum, "given", row, row)
+            if reversed_partner(row) >= OFFLOADED:
+                add_term(left_sum, "left", reversed_partner(row), row)
+
+        offload_term(0)
+        offload_term(1)
+        use_row(0)
+        use_row(1)
 
         neg_max = held.tile([P, BLOCKS], F32, name="neg_max")
         expd = held.tile([P, BLOCKS, S], F32, name="expd")
@@ -181,9 +177,10 @@ def tile_hungarianmatcherpolyline_kernel(tc, logits, pred_poly, tgt_poly, offs, 
                 out=lost[:, b, cols], in0=b_lo[:, cols], scalar=a_lo[:, b, d : d + 1],
                 in1=above[:, b, cols], op0=ALU.max, op1=ALU.add,
             )
-        offload_point(1)
-        for d in range(XY):
-            add_terms(given_sum, "given", 3, 3, d)
+        offload_term(2)
+        offload_term(3)
+        use_row(6)
+        use_row(7)
         for b, d, cols in sides:
             nc.scalar.activation(
                 out=overlap[:, b, cols], in_=lost[:, b, cols], func=FN.Relu, bias=a_hi[:, b, d : d + 1], scale=-1.0
@@ -193,7 +190,7 @@ def tile_hungarianmatcherpolyline_kernel(tc, logits, pred_poly, tgt_poly, offs, 
                 out=extent[:, b, cols], in0=lost[:, b, cols], scalar=a_lo[:, b, d : d + 1],
                 in1=b_side[:, cols], op0=ALU.subtract, op1=ALU.add,
             )
-        offload_point(2)
+        offload_term(4)
         hull, hull_floor, hull_root, hull_inv = (per_block(f"hull{s}") for s in ("", "_floor", "_root", "_inv"))
         union, union_floor, union_root, union_inv = (per_block(f"union{s}") for s in ("", "_floor", "_root", "_inv"))
         inter = per_block("inter")
@@ -202,10 +199,10 @@ def tile_hungarianmatcherpolyline_kernel(tc, logits, pred_poly, tgt_poly, offs, 
             nc.vector.tensor_mul(hull[:, b, :], extent[:, b, x_cols], extent[:, b, y_cols])
         for b in range(BLOCKS):
             nc.vector.tensor_scalar_max(hull_floor[:, b, :], hull[:, b, :], EPS)
-        add_terms(given_sum, "given", 2, 2, 0)
+        use_row(4)
         for b in range(BLOCKS):
             nc.vector.tensor_mul(inter[:, b, :], overlap[:, b, x_cols], overlap[:, b, y_cols])
-        add_terms(given_sum, "given", 2, 2, 1)
+        use_row(5)
         for b in range(BLOCKS):
             nc.vector.scalar_tensor_tensor(
                 out=union[:, b, :], in0=area2[:], scalar=area1[:, b : b + 1], in1=inter[:, b, :],
@@ -223,13 +220,13 @@ def tile_hungarianmatcherpolyline_kernel(tc, logits, pred_poly, tgt_poly, offs, 
                 nc.scalar.activation(out=inv[:, b, :], in_=root[:, b, :], func=FN.Square)
 
         invert(hull_floor, hull_root, hull_inv)
-        add_terms(given_sum, "given", 1, 1, 0)
+        use_row(2)
         for b in range(BLOCKS):
             nc.vector.tensor_scalar_max(union_floor[:, b, :], union[:, b, :], EPS)
         invert(union_floor, union_root, union_inv)
         for b in range(BLOCKS):
             nc.vector.tensor_sub(excess[:, b, :], hull[:, b, :], union[:, b, :])
-        add_terms(given_sum, "given", 1, 1, 1)
+        use_row(3)
 
         inv_total = held.tile([P, BLOCKS], F32, name="inv_total")
         neg_prob = [held.tile([P, S], F32, name=f"neg_prob{b}") for b in range(BLOCKS)]
@@ -243,15 +240,24 @@ def tile_hungarianmatcherpolyline_kernel(tc, logits, pred_poly, tgt_poly, offs, 
         for b in range(BLOCKS):
             nc.vector.tensor_tensor(picked[b][:], neg_prob[b][:].indirect(offsets[:]), tgt_term[:], ALU.add)
 
-        reversed_sum = per_block("reversed_sum")
-        best = per_block("best")
-        with_poly = per_block("with_poly")
         excess_ratio = per_block("excess_ratio")
         inter_ratio = per_block("inter_ratio")
         with_excess = per_block("with_excess")
+        all_but_min = per_block("all_but_min")
+        reversed_sum = per_block("reversed_sum")
+        best = per_block("best")
         cost = [held.tile([P, N], F32, name=f"cost{b}") for b in range(BLOCKS)]
         for b in range(BLOCKS):
             nc.vector.tensor_mul(excess_ratio[:, b, :], excess[:, b, :], hull_inv[:, b, :])
+        for b in range(BLOCKS):
+            nc.vector.scalar_tensor_tensor(
+                out=with_excess[:, b, :], in0=picked[b][:], scalar=pred_term[:, b : b + 1],
+                in1=excess_ratio[:, b, :], op0=ALU.add, op1=ALU.add,
+            )
+        for b in range(BLOCKS):
+            nc.vector.tensor_mul(inter_ratio[:, b, :], inter[:, b, :], union_inv[:, b, :])
+        for b in range(BLOCKS):
+            nc.vector.tensor_sub(all_but_min[:, b, :], with_excess[:, b, :], inter_ratio[:, b, :])
         for b in range(BLOCKS):
             nc.vector.scalar_tensor_tensor(
                 out=reversed_sum[:, b, :], in0=block(offloaded_terms, b), scalar=offloaded_sum[:, b : b + 1],
@@ -259,18 +265,9 @@ def tile_hungarianmatcherpolyline_kernel(tc, logits, pred_poly, tgt_poly, offs, 
             )
         for b in range(BLOCKS):
             nc.vector.tensor_tensor(best[:, b, :], reversed_sum[:, b, :], given_sum[b], ALU.min)
-        for b in range(BLOCKS):
+        for b, queue in enumerate((nc.sync, nc.scalar)):
             nc.vector.scalar_tensor_tensor(
-                out=with_poly[:, b, :], in0=best[:, b, :], scalar=1.25, in1=picked[b][:],
+                out=cost[b][:], in0=best[:, b, :], scalar=1.25, in1=all_but_min[:, b, :],
                 op0=ALU.mult, op1=ALU.add,
             )
-        for b in range(BLOCKS):
-            nc.vector.scalar_tensor_tensor(
-                out=with_excess[:, b, :], in0=with_poly[:, b, :], scalar=pred_term[:, b : b + 1],
-                in1=excess_ratio[:, b, :], op0=ALU.add, op1=ALU.add,
-            )
-        for b in range(BLOCKS):
-            nc.vector.tensor_mul(inter_ratio[:, b, :], inter[:, b, :], union_inv[:, b, :])
-        for b, queue in enumerate((nc.sync, nc.scalar)):
-            nc.vector.tensor_sub(cost[b][:], with_excess[:, b, :], inter_ratio[:, b, :])
             queue.dma_start(out.rearrange("(p b) j -> p b j", b=BLOCKS)[:, b, :], cost[b][:])

@@ -96,22 +96,6 @@ def tile_hungarianmatcherpolyline_kernel(tc, logits, pred_poly, tgt_poly, offs, 
         nc.vector.tensor_reduce(out=pred_sum[:], in_=pred[:], axis=X, op=ALU.add)
         nc.vector.tensor_scalar_mul(pred_term[:], pred_sum[:], -0.625)
 
-        def spread(columns, coords, name):
-            row = psum.tile([P, coords * N], F32, name=name)
-            for d in range(coords):
-                for h in range(HALVES):
-                    first = d * N + h * P
-                    nc.tensor.transpose(
-                        row[:, first : first + P], columns[:, d, h : h + 1].to_broadcast([P, P]), ident[:]
-                    )
-            return row
-
-        b_hi = spread(col_hi, XY, "b_hi")
-        b_lo = spread(col_lo, XY, "b_lo")
-        b_side = spread(col_side, XY, "b_side")
-        area2 = spread(col_area, 1, "area2")
-        tgt_sum = spread(col_sum, 1, "tgt_sum")
-
         offloaded_terms = psum.tile([P, BLOCKS * N], F32, name="offloaded_terms")
 
         def offload_term(c):
@@ -143,15 +127,47 @@ def tile_hungarianmatcherpolyline_kernel(tc, logits, pred_poly, tgt_poly, offs, 
             if reversed_partner(row) >= OFFLOADED:
                 add_term(left_sum, "left", reversed_partner(row), row)
 
-        offload_term(0)
-        offload_term(1)
         use_row(0)
         use_row(1)
+
+        def spread(columns, coords, name):
+            row = psum.tile([P, coords * N], F32, name=name)
+            for d in range(coords):
+                for h in range(HALVES):
+                    first = d * N + h * P
+                    nc.tensor.transpose(
+                        row[:, first : first + P], columns[:, d, h : h + 1].to_broadcast([P, P]), ident[:]
+                    )
+            return row
+
+        b_hi = spread(col_hi, XY, "b_hi")
+        b_lo = spread(col_lo, XY, "b_lo")
+        b_side = spread(col_side, XY, "b_side")
+        area2 = spread(col_area, 1, "area2")
+        tgt_sum = spread(col_sum, 1, "tgt_sum")
+
+        offload_term(0)
+        offload_term(1)
 
         neg_max = held.tile([P, BLOCKS], F32, name="neg_max")
         expd = held.tile([P, BLOCKS, S], F32, name="expd")
         total = held.tile([P, BLOCKS], F32, name="total")
         nc.vector.tensor_reduce(out=neg_max[:], in_=scores[:], axis=X, op=ALU.max, negate=True)
+        for b in range(BLOCKS):
+            nc.scalar.activation(
+                out=expd[:, b, :], in_=scores[:, b, :], func=FN.Exp, bias=neg_max[:, b : b + 1], scale=1.0,
+                accum_out=total[:, b : b + 1],
+            )
+
+        use_row(6)
+        use_row(7)
+        offload_term(2)
+        offload_term(3)
+        use_row(4)
+        use_row(5)
+        offload_term(4)
+        use_row(2)
+        use_row(3)
 
         above = held.tile([P, BLOCKS, XY * N], F32, name="above")
         lost = held.tile([P, BLOCKS, XY * N], F32, name="lost")
@@ -163,24 +179,20 @@ def tile_hungarianmatcherpolyline_kernel(tc, logits, pred_poly, tgt_poly, offs, 
         def per_block(name):
             return held.tile([P, BLOCKS, N], F32, name=name)
 
+        hull, hull_floor, hull_root, hull_inv = (per_block(f"hull{s}") for s in ("", "_floor", "_root", "_inv"))
+        union, union_floor, union_root, union_inv = (per_block(f"union{s}") for s in ("", "_floor", "_root", "_inv"))
+        inter = per_block("inter")
+        excess = per_block("excess")
+
         for b, d, cols in sides:
             nc.scalar.activation(
                 out=above[:, b, cols], in_=b_hi[:, cols], func=FN.Relu, bias=a_hi[:, b, d : d + 1], scale=-1.0
-            )
-        for b in range(BLOCKS):
-            nc.scalar.activation(
-                out=expd[:, b, :], in_=scores[:, b, :], func=FN.Exp, bias=neg_max[:, b : b + 1], scale=1.0,
-                accum_out=total[:, b : b + 1],
             )
         for b, d, cols in sides:
             nc.vector.scalar_tensor_tensor(
                 out=lost[:, b, cols], in0=b_lo[:, cols], scalar=a_lo[:, b, d : d + 1],
                 in1=above[:, b, cols], op0=ALU.max, op1=ALU.add,
             )
-        offload_term(2)
-        offload_term(3)
-        use_row(6)
-        use_row(7)
         for b, d, cols in sides:
             nc.scalar.activation(
                 out=overlap[:, b, cols], in_=lost[:, b, cols], func=FN.Relu, bias=a_hi[:, b, d : d + 1], scale=-1.0
@@ -190,19 +202,12 @@ def tile_hungarianmatcherpolyline_kernel(tc, logits, pred_poly, tgt_poly, offs, 
                 out=extent[:, b, cols], in0=lost[:, b, cols], scalar=a_lo[:, b, d : d + 1],
                 in1=b_side[:, cols], op0=ALU.subtract, op1=ALU.add,
             )
-        offload_term(4)
-        hull, hull_floor, hull_root, hull_inv = (per_block(f"hull{s}") for s in ("", "_floor", "_root", "_inv"))
-        union, union_floor, union_root, union_inv = (per_block(f"union{s}") for s in ("", "_floor", "_root", "_inv"))
-        inter = per_block("inter")
-        excess = per_block("excess")
         for b in range(BLOCKS):
             nc.vector.tensor_mul(hull[:, b, :], extent[:, b, x_cols], extent[:, b, y_cols])
         for b in range(BLOCKS):
             nc.vector.tensor_scalar_max(hull_floor[:, b, :], hull[:, b, :], EPS)
-        use_row(4)
         for b in range(BLOCKS):
             nc.vector.tensor_mul(inter[:, b, :], overlap[:, b, x_cols], overlap[:, b, y_cols])
-        use_row(5)
         for b in range(BLOCKS):
             nc.vector.scalar_tensor_tensor(
                 out=union[:, b, :], in0=area2[:], scalar=area1[:, b : b + 1], in1=inter[:, b, :],
@@ -220,13 +225,11 @@ def tile_hungarianmatcherpolyline_kernel(tc, logits, pred_poly, tgt_poly, offs, 
                 nc.scalar.activation(out=inv[:, b, :], in_=root[:, b, :], func=FN.Square)
 
         invert(hull_floor, hull_root, hull_inv)
-        use_row(2)
         for b in range(BLOCKS):
             nc.vector.tensor_scalar_max(union_floor[:, b, :], union[:, b, :], EPS)
         invert(union_floor, union_root, union_inv)
         for b in range(BLOCKS):
             nc.vector.tensor_sub(excess[:, b, :], hull[:, b, :], union[:, b, :])
-        use_row(3)
 
         inv_total = held.tile([P, BLOCKS], F32, name="inv_total")
         neg_prob = [held.tile([P, S], F32, name=f"neg_prob{b}") for b in range(BLOCKS)]

@@ -14,7 +14,7 @@ ROWS = K * XY
 BLOCKS = Q // P
 HALVES = N // P
 EPS = 1e-6
-OFFLOADED = 5
+OFFLOADED = 4
 
 
 def reversed_partner(c):
@@ -165,7 +165,6 @@ def tile_hungarianmatcherpolyline_kernel(tc, logits, pred_poly, tgt_poly, offs, 
         offload_term(3)
         use_row(4)
         use_row(5)
-        offload_term(4)
         use_row(2)
         use_row(3)
 

@@ -55,6 +55,8 @@ def tile_hungarianmatcherpolyline_kernel(tc, logits, pred_poly, tgt_poly, offs, 
 
         ident = held.tile([P, P], F32, name="ident")
         make_identity(nc, ident[:])
+        sum_weights = held.tile([ROWS, P], F32, name="sum_weights")
+        nc.vector.memset(sum_weights[:], -0.625)
         dummy = held.tile([P, 1], F32, name="dummy")
         nc.vector.memset(dummy[:], 0.0)
         warmed = held.tile([P, 1], F32, name="warmed")
@@ -65,6 +67,10 @@ def tile_hungarianmatcherpolyline_kernel(tc, logits, pred_poly, tgt_poly, offs, 
             nc.tensor.matmul(
                 tgt_t[:, h, :], tgt_rows[:, h * P : (h + 1) * P], ident[0:ROWS, 0:ROWS], start=True, stop=True
             )
+        tgt_sum = psum.tile([P, N], F32, name="tgt_sum")
+        nc.tensor.matmul(tgt_sum[:], sum_weights[:], tgt_rows[:], start=True, stop=True)
+        tgt_term = held.tile([P, N], F32, name="tgt_term")
+        nc.scalar.activation(out=tgt_term[:], in_=tgt_sum[:], func=FN.Copy)
         tgt_points_last = tgt_t[:].rearrange("p h (k d) -> p d h k", d=XY)
         pred_points_last = pred[:].rearrange("p b (k d) -> p b d k", d=XY)
 
@@ -72,7 +78,6 @@ def tile_hungarianmatcherpolyline_kernel(tc, logits, pred_poly, tgt_poly, offs, 
         col_lo = held.tile([P, XY, HALVES], F32, name="col_lo")
         col_side = held.tile([P, XY, HALVES], F32, name="col_side")
         col_area = held.tile([P, 1, HALVES], F32, name="col_area")
-        col_sum = held.tile([P, 1, HALVES], F32, name="col_sum")
         neg_pred = held.tile([P, BLOCKS, ROWS], F32, name="neg_pred")
         a_hi = held.tile([P, BLOCKS, XY], F32, name="a_hi")
         a_lo = held.tile([P, BLOCKS, XY], F32, name="a_lo")
@@ -88,7 +93,6 @@ def tile_hungarianmatcherpolyline_kernel(tc, logits, pred_poly, tgt_poly, offs, 
         nc.vector.tensor_reduce(out=a_hi[:], in_=pred_points_last, axis=X, op=ALU.max)
         nc.vector.tensor_reduce(out=a_lo[:], in_=pred_points_last, axis=X, op=ALU.min)
         nc.vector.tensor_sub(col_side[:], col_hi[:], col_lo[:])
-        nc.vector.tensor_reduce(out=col_sum[:, 0, :], in_=tgt_t[:], axis=X, op=ALU.add)
         nc.vector.tensor_sub(a_side[:], a_hi[:], a_lo[:])
         nc.vector.tensor_mul(col_area[:, 0, :], col_side[:, 0, :], col_side[:, 1, :])
         nc.vector.tensor_mul(area1[:], a_side[:, :, 0], a_side[:, :, 1])
@@ -144,7 +148,6 @@ def tile_hungarianmatcherpolyline_kernel(tc, logits, pred_poly, tgt_poly, offs, 
         b_lo = spread(col_lo, XY, "b_lo")
         b_side = spread(col_side, XY, "b_side")
         area2 = spread(col_area, 1, "area2")
-        tgt_sum = spread(col_sum, 1, "tgt_sum")
 
         offload_term(0)
         offload_term(1)
@@ -167,6 +170,18 @@ def tile_hungarianmatcherpolyline_kernel(tc, logits, pred_poly, tgt_poly, offs, 
         use_row(5)
         use_row(2)
         use_row(3)
+
+        inv_total = held.tile([P, BLOCKS], F32, name="inv_total")
+        neg_prob = [held.tile([P, S], F32, name=f"neg_prob{b}") for b in range(BLOCKS)]
+        picked = [held.tile([P, N], F32, name=f"picked{b}") for b in range(BLOCKS)]
+        nc.vector.reciprocal(inv_total[:], total[:])
+        for b in range(BLOCKS):
+            nc.vector.tensor_scalar(
+                out=neg_prob[b][:], in0=expd[:, b, :], scalar1=inv_total[:, b : b + 1], scalar2=-1.0,
+                op0=ALU.mult, op1=ALU.mult,
+            )
+        for b in range(BLOCKS):
+            nc.vector.tensor_tensor(picked[b][:], neg_prob[b][:].indirect(offsets[:]), tgt_term[:], ALU.add)
 
         above = held.tile([P, BLOCKS, XY * N], F32, name="above")
         lost = held.tile([P, BLOCKS, XY * N], F32, name="lost")
@@ -213,8 +228,6 @@ def tile_hungarianmatcherpolyline_kernel(tc, logits, pred_poly, tgt_poly, offs, 
                 op0=ALU.add, op1=ALU.subtract,
             )
 
-        tgt_term = held.tile([P, N], F32, name="tgt_term")
-        nc.scalar.activation(out=tgt_term[:], in_=tgt_sum[:], func=FN.Copy, scale=-0.625)
         nc.scalar.activation(out=warmed[:], in_=total[:, BLOCKS - 1 : BLOCKS], func=FN.Abs_reciprocal_sqrt)
 
         def invert(floor, root, inv):
@@ -229,18 +242,6 @@ def tile_hungarianmatcherpolyline_kernel(tc, logits, pred_poly, tgt_poly, offs, 
         invert(union_floor, union_root, union_inv)
         for b in range(BLOCKS):
             nc.vector.tensor_sub(excess[:, b, :], hull[:, b, :], union[:, b, :])
-
-        inv_total = held.tile([P, BLOCKS], F32, name="inv_total")
-        neg_prob = [held.tile([P, S], F32, name=f"neg_prob{b}") for b in range(BLOCKS)]
-        picked = [held.tile([P, N], F32, name=f"picked{b}") for b in range(BLOCKS)]
-        nc.vector.reciprocal(inv_total[:], total[:])
-        for b in range(BLOCKS):
-            nc.vector.tensor_scalar(
-                out=neg_prob[b][:], in0=expd[:, b, :], scalar1=inv_total[:, b : b + 1], scalar2=-1.0,
-                op0=ALU.mult, op1=ALU.mult,
-            )
-        for b in range(BLOCKS):
-            nc.vector.tensor_tensor(picked[b][:], neg_prob[b][:].indirect(offsets[:]), tgt_term[:], ALU.add)
 
         excess_ratio = per_block("excess_ratio")
         inter_ratio = per_block("inter_ratio")

@@ -14,7 +14,7 @@ ROWS = K * XY
 BLOCKS = Q // P
 HALVES = N // P
 EPS = 1e-6
-OFFLOADED = 4
+OFFLOADED = 5
 
 
 def reversed_partner(c):
@@ -101,6 +101,8 @@ def tile_hungarianmatcherpolyline_kernel(tc, logits, pred_poly, tgt_poly, offs, 
         nc.vector.tensor_scalar_mul(pred_term[:], pred_sum[:], -0.625)
 
         offloaded_terms = psum.tile([P, BLOCKS * N], F32, name="offloaded_terms")
+        given_sum = [None for b in range(BLOCKS)]
+        left_sum = [None for b in range(BLOCKS)]
 
         def offload_term(c):
             term = held.tile([P, BLOCKS * N], F32, name=f"term{c}")
@@ -109,28 +111,31 @@ def tile_hungarianmatcherpolyline_kernel(tc, logits, pred_poly, tgt_poly, offs, 
                     out=block(term, b), in_=tgt[:, reversed_partner(c), :], func=FN.Relu,
                     bias=neg_pred[:, b, c : c + 1], scale=1.0,
                 )
-            nc.tensor.matmul(offloaded_terms[:], ident[:], term[:], start=(c == 0), stop=(c == OFFLOADED - 1))
+            if c == 0:
+                for b in range(BLOCKS):
+                    left_sum[b] = block(term, b)
+            else:
+                nc.tensor.matmul(offloaded_terms[:], ident[:], term[:], start=(c == 1), stop=False)
 
         def add_term(sums, label, c, row):
+            longer = held.tile([P, BLOCKS * N], F32, name=f"{label}{c}")
             for b in range(BLOCKS):
-                longer = held.tile([P, N], F32, name=f"{label}{b}{c}")
                 if sums[b] is None:
-                    nc.vector.tensor_scalar_max(longer[:], tgt[:, row, :], pred[:, b, c : c + 1])
+                    nc.vector.tensor_scalar_max(block(longer, b), tgt[:, row, :], pred[:, b, c : c + 1])
                 else:
                     nc.vector.scalar_tensor_tensor(
-                        out=longer[:], in0=tgt[:, row, :], scalar=pred[:, b, c : c + 1],
+                        out=block(longer, b), in0=tgt[:, row, :], scalar=pred[:, b, c : c + 1],
                         in1=sums[b], op0=ALU.max, op1=ALU.add,
                     )
-                sums[b] = longer[:]
-
-        given_sum = [None for b in range(BLOCKS)]
-        left_sum = [None for b in range(BLOCKS)]
+                sums[b] = block(longer, b)
+            return longer
 
         def use_row(row):
             add_term(given_sum, "given", row, row)
             if reversed_partner(row) >= OFFLOADED:
-                add_term(left_sum, "left", reversed_partner(row), row)
+                return add_term(left_sum, "left", reversed_partner(row), row)
 
+        offload_term(0)
         use_row(0)
         use_row(1)
 
@@ -149,17 +154,13 @@ def tile_hungarianmatcherpolyline_kernel(tc, logits, pred_poly, tgt_poly, offs, 
         b_side = spread(col_side, XY, "b_side")
         area2 = spread(col_area, 1, "area2")
 
-        offload_term(0)
         offload_term(1)
 
-        neg_max = held.tile([P, BLOCKS], F32, name="neg_max")
         expd = held.tile([P, BLOCKS, S], F32, name="expd")
         total = held.tile([P, BLOCKS], F32, name="total")
-        nc.vector.tensor_reduce(out=neg_max[:], in_=scores[:], axis=X, op=ALU.max, negate=True)
         for b in range(BLOCKS):
             nc.scalar.activation(
-                out=expd[:, b, :], in_=scores[:, b, :], func=FN.Exp, bias=neg_max[:, b : b + 1], scale=1.0,
-                accum_out=total[:, b : b + 1],
+                out=expd[:, b, :], in_=scores[:, b, :], func=FN.Exp, accum_out=total[:, b : b + 1],
             )
 
         use_row(6)
@@ -168,8 +169,10 @@ def tile_hungarianmatcherpolyline_kernel(tc, logits, pred_poly, tgt_poly, offs, 
         offload_term(3)
         use_row(4)
         use_row(5)
+        offload_term(4)
         use_row(2)
-        use_row(3)
+        left_total = use_row(3)
+        nc.tensor.matmul(offloaded_terms[:], ident[:], left_total[:], start=False, stop=True)
 
         inv_total = held.tile([P, BLOCKS], F32, name="inv_total")
         neg_prob = [held.tile([P, S], F32, name=f"neg_prob{b}") for b in range(BLOCKS)]
@@ -193,8 +196,8 @@ def tile_hungarianmatcherpolyline_kernel(tc, logits, pred_poly, tgt_poly, offs, 
         def per_block(name):
             return held.tile([P, BLOCKS, N], F32, name=name)
 
-        hull, hull_floor, hull_root, hull_inv = (per_block(f"hull{s}") for s in ("", "_floor", "_root", "_inv"))
-        union, union_floor, union_root, union_inv = (per_block(f"union{s}") for s in ("", "_floor", "_root", "_inv"))
+        hull, hull_root, hull_inv = (per_block(f"hull{s}") for s in ("", "_root", "_inv"))
+        union, union_root, union_inv = (per_block(f"union{s}") for s in ("", "_root", "_inv"))
         inter = per_block("inter")
         excess = per_block("excess")
 
@@ -219,8 +222,6 @@ def tile_hungarianmatcherpolyline_kernel(tc, logits, pred_poly, tgt_poly, offs, 
         for b in range(BLOCKS):
             nc.vector.tensor_mul(hull[:, b, :], extent[:, b, x_cols], extent[:, b, y_cols])
         for b in range(BLOCKS):
-            nc.vector.tensor_scalar_max(hull_floor[:, b, :], hull[:, b, :], EPS)
-        for b in range(BLOCKS):
             nc.vector.tensor_mul(inter[:, b, :], overlap[:, b, x_cols], overlap[:, b, y_cols])
         for b in range(BLOCKS):
             nc.vector.scalar_tensor_tensor(
@@ -230,16 +231,14 @@ def tile_hungarianmatcherpolyline_kernel(tc, logits, pred_poly, tgt_poly, offs, 
 
         nc.scalar.activation(out=warmed[:], in_=total[:, BLOCKS - 1 : BLOCKS], func=FN.Abs_reciprocal_sqrt)
 
-        def invert(floor, root, inv):
+        def invert(area, root, inv):
             for b in range(BLOCKS):
-                nc.scalar.activation(out=root[:, b, :], in_=floor[:, b, :], func=FN.Abs_reciprocal_sqrt)
+                nc.scalar.activation(out=root[:, b, :], in_=area[:, b, :], func=FN.Abs_reciprocal_sqrt)
             for b in range(BLOCKS):
                 nc.scalar.activation(out=inv[:, b, :], in_=root[:, b, :], func=FN.Square)
 
-        invert(hull_floor, hull_root, hull_inv)
-        for b in range(BLOCKS):
-            nc.vector.tensor_scalar_max(union_floor[:, b, :], union[:, b, :], EPS)
-        invert(union_floor, union_root, union_inv)
+        invert(hull, hull_root, hull_inv)
+        invert(union, union_root, union_inv)
         for b in range(BLOCKS):
             nc.vector.tensor_sub(excess[:, b, :], hull[:, b, :], union[:, b, :])
 
@@ -247,27 +246,30 @@ def tile_hungarianmatcherpolyline_kernel(tc, logits, pred_poly, tgt_poly, offs, 
         inter_ratio = per_block("inter_ratio")
         with_excess = per_block("with_excess")
         all_but_min = per_block("all_but_min")
-        reversed_sum = per_block("reversed_sum")
         best = per_block("best")
         cost = [held.tile([P, N], F32, name=f"cost{b}") for b in range(BLOCKS)]
         for b in range(BLOCKS):
-            nc.vector.tensor_mul(excess_ratio[:, b, :], excess[:, b, :], hull_inv[:, b, :])
+            nc.vector.scalar_tensor_tensor(
+                out=excess_ratio[:, b, :], in0=hull_inv[:, b, :], scalar=1.0 / EPS, in1=excess[:, b, :],
+                op0=ALU.min, op1=ALU.mult,
+            )
         for b in range(BLOCKS):
             nc.vector.scalar_tensor_tensor(
                 out=with_excess[:, b, :], in0=picked[b][:], scalar=pred_term[:, b : b + 1],
                 in1=excess_ratio[:, b, :], op0=ALU.add, op1=ALU.add,
             )
         for b in range(BLOCKS):
-            nc.vector.tensor_mul(inter_ratio[:, b, :], inter[:, b, :], union_inv[:, b, :])
+            nc.vector.scalar_tensor_tensor(
+                out=inter_ratio[:, b, :], in0=union_inv[:, b, :], scalar=1.0 / EPS, in1=inter[:, b, :],
+                op0=ALU.min, op1=ALU.mult,
+            )
         for b in range(BLOCKS):
             nc.vector.tensor_sub(all_but_min[:, b, :], with_excess[:, b, :], inter_ratio[:, b, :])
         for b in range(BLOCKS):
             nc.vector.scalar_tensor_tensor(
-                out=reversed_sum[:, b, :], in0=block(offloaded_terms, b), scalar=offloaded_sum[:, b : b + 1],
-                in1=left_sum[b], op0=ALU.add, op1=ALU.add,
+                out=best[:, b, :], in0=block(offloaded_terms, b), scalar=offloaded_sum[:, b : b + 1],
+                in1=given_sum[b], op0=ALU.add, op1=ALU.min,
             )
-        for b in range(BLOCKS):
-            nc.vector.tensor_tensor(best[:, b, :], reversed_sum[:, b, :], given_sum[b], ALU.min)
         for b, queue in enumerate((nc.sync, nc.scalar)):
             nc.vector.scalar_tensor_tensor(
                 out=cost[b][:], in0=best[:, b, :], scalar=1.25, in1=all_but_min[:, b, :],

@@ -245,7 +245,7 @@ def tile_hungarianmatcherpolyline_kernel(tc, logits, pred_poly, tgt_poly, offs, 
         excess_ratio = per_block("excess_ratio")
         inter_ratio = per_block("inter_ratio")
         with_excess = per_block("with_excess")
-        all_but_min = per_block("all_but_min")
+        all_but_inter = per_block("all_but_inter")
         best = per_block("best")
         cost = [held.tile([P, N], F32, name=f"cost{b}") for b in range(BLOCKS)]
         for b in range(BLOCKS):
@@ -260,19 +260,19 @@ def tile_hungarianmatcherpolyline_kernel(tc, logits, pred_poly, tgt_poly, offs, 
             )
         for b in range(BLOCKS):
             nc.vector.scalar_tensor_tensor(
-                out=inter_ratio[:, b, :], in0=union_inv[:, b, :], scalar=1.0 / EPS, in1=inter[:, b, :],
-                op0=ALU.min, op1=ALU.mult,
-            )
-        for b in range(BLOCKS):
-            nc.vector.tensor_sub(all_but_min[:, b, :], with_excess[:, b, :], inter_ratio[:, b, :])
-        for b in range(BLOCKS):
-            nc.vector.scalar_tensor_tensor(
                 out=best[:, b, :], in0=block(offloaded_terms, b), scalar=offloaded_sum[:, b : b + 1],
                 in1=given_sum[b], op0=ALU.add, op1=ALU.min,
             )
-        for b, queue in enumerate((nc.sync, nc.scalar)):
+        for b in range(BLOCKS):
             nc.vector.scalar_tensor_tensor(
-                out=cost[b][:], in0=best[:, b, :], scalar=1.25, in1=all_but_min[:, b, :],
+                out=all_but_inter[:, b, :], in0=best[:, b, :], scalar=1.25, in1=with_excess[:, b, :],
                 op0=ALU.mult, op1=ALU.add,
             )
+        for b in range(BLOCKS):
+            nc.vector.scalar_tensor_tensor(
+                out=inter_ratio[:, b, :], in0=union_inv[:, b, :], scalar=1.0 / EPS, in1=inter[:, b, :],
+                op0=ALU.min, op1=ALU.mult,
+            )
+        for b, queue in enumerate((nc.sync, nc.scalar)):
+            nc.vector.tensor_sub(cost[b][:], all_but_inter[:, b, :], inter_ratio[:, b, :])
             queue.dma_start(out.rearrange("(p b) j -> p b j", b=BLOCKS)[:, b, :], cost[b][:])

@@ -14,7 +14,8 @@ ROWS = K * XY
 BLOCKS = Q // P
 HALVES = N // P
 EPS = 1e-6
-OFFLOADED = 5
+ROW_ORDER = (6, 7, 0, 1, 4, 5, 2, 3)
+SCALAR_ROWS = 4
 
 
 def reversed_partner(c):
@@ -25,10 +26,13 @@ def tile_hungarianmatcherpolyline_kernel(tc, logits, pred_poly, tgt_poly, offs, 
     nc = tc.nc
     with tc.tile_pool(name="held", bufs=1) as held, tc.psum_pool(name="psum", bufs=1) as psum:
         tgt_rows = held.tile([ROWS, N], F32, name="tgt_rows")
-        nc.scalar.dma_start(tgt_rows[:], tgt_poly)
+        nc.sync.dma_start(tgt_rows[:], tgt_poly)
 
         pred = held.tile([P, BLOCKS, ROWS], F32, name="pred")
-        nc.sync.dma_start(pred[:], pred_poly.rearrange("(p b) c -> p b c", b=BLOCKS))
+        nc.scalar.dma_start(pred[:], pred_poly.rearrange("(p b) c -> p b c", b=BLOCKS))
+
+        scores = held.tile([P, BLOCKS, S], F32, name="scores")
+        nc.sync.dma_start(scores[:], logits.rearrange("(p b) s -> p b s", b=BLOCKS))
 
         tgt = held.tile([P, ROWS, N], F32, name="tgt")
 
@@ -40,121 +44,102 @@ def tile_hungarianmatcherpolyline_kernel(tc, logits, pred_poly, tgt_poly, offs, 
             )
 
         for d in range(XY):
-            load_rows(0 * XY + d, 1, nc.sync)
             load_rows(3 * XY + d, 1, nc.scalar)
+            load_rows(0 * XY + d, 1, nc.sync)
         load_rows(2 * XY, XY, nc.scalar)
-        scores = held.tile([P, BLOCKS, S], F32, name="scores")
-        nc.sync.dma_start(scores[:], logits.rearrange("(p b) s -> p b s", b=BLOCKS))
         load_rows(1 * XY, XY, nc.sync)
 
         offsets = held.tile([P, N // 16], U16, name="offsets")
         nc.sync.dma_start(offsets[:], offs)
 
-        def block(tile, b):
-            return tile[:, b * N : (b + 1) * N]
-
         ident = held.tile([P, P], F32, name="ident")
         make_identity(nc, ident[:])
-        sum_weights = held.tile([ROWS, P], F32, name="sum_weights")
-        nc.vector.memset(sum_weights[:], -0.625)
         dummy = held.tile([P, 1], F32, name="dummy")
         nc.vector.memset(dummy[:], 0.0)
         warmed = held.tile([P, 1], F32, name="warmed")
         nc.scalar.activation(out=warmed[:], in_=dummy[:], func=FN.Exp)
 
-        tgt_t = psum.tile([P, HALVES, ROWS], F32, name="tgt_t")
-        for h in range(HALVES):
+        def add_flipped(total, first_columns, tile, columns, start, stop):
             nc.tensor.matmul(
-                tgt_t[:, h, :], tgt_rows[:, h * P : (h + 1) * P], ident[0:ROWS, 0:ROWS], start=True, stop=True
+                total[:, first_columns : first_columns + P], tile[:, columns], ident[:],
+                is_transpose=True, start=start, stop=stop,
             )
-        tgt_sum = psum.tile([P, N], F32, name="tgt_sum")
-        nc.tensor.matmul(tgt_sum[:], sum_weights[:], tgt_rows[:], start=True, stop=True)
-        tgt_term = held.tile([P, N], F32, name="tgt_term")
-        nc.scalar.activation(out=tgt_term[:], in_=tgt_sum[:], func=FN.Copy)
-        tgt_points_last = tgt_t[:].rearrange("p h (k d) -> p d h k", d=XY)
-        pred_points_last = pred[:].rearrange("p b (k d) -> p b d k", d=XY)
 
-        col_hi = held.tile([P, XY, HALVES], F32, name="col_hi")
-        col_lo = held.tile([P, XY, HALVES], F32, name="col_lo")
-        col_side = held.tile([P, XY, HALVES], F32, name="col_side")
-        col_area = held.tile([P, 1, HALVES], F32, name="col_area")
         neg_pred = held.tile([P, BLOCKS, ROWS], F32, name="neg_pred")
         a_hi = held.tile([P, BLOCKS, XY], F32, name="a_hi")
         a_lo = held.tile([P, BLOCKS, XY], F32, name="a_lo")
         a_side = held.tile([P, BLOCKS, XY], F32, name="a_side")
-        area1 = held.tile([P, BLOCKS], F32, name="area1")
+        area1 = held.tile([P, BLOCKS, 1], F32, name="area1")
         pred_sum = held.tile([P, BLOCKS], F32, name="pred_sum")
         pred_term = held.tile([P, BLOCKS], F32, name="pred_term")
-        offloaded_sum = held.tile([P, BLOCKS], F32, name="offloaded_sum")
-
-        nc.vector.tensor_reduce(out=col_hi[:], in_=tgt_points_last, axis=X, op=ALU.max)
-        nc.vector.tensor_reduce(out=col_lo[:], in_=tgt_points_last, axis=X, op=ALU.min)
+        pred_points_last = pred[:].rearrange("p b (k d) -> p b d k", d=XY)
         nc.vector.tensor_scalar_mul(neg_pred[:], pred[:], -1.0)
         nc.vector.tensor_reduce(out=a_hi[:], in_=pred_points_last, axis=X, op=ALU.max)
         nc.vector.tensor_reduce(out=a_lo[:], in_=pred_points_last, axis=X, op=ALU.min)
-        nc.vector.tensor_sub(col_side[:], col_hi[:], col_lo[:])
         nc.vector.tensor_sub(a_side[:], a_hi[:], a_lo[:])
-        nc.vector.tensor_mul(col_area[:, 0, :], col_side[:, 0, :], col_side[:, 1, :])
-        nc.vector.tensor_mul(area1[:], a_side[:, :, 0], a_side[:, :, 1])
-        nc.vector.tensor_reduce(out=offloaded_sum[:], in_=pred[:, :, 0:OFFLOADED], axis=X, op=ALU.add)
+        nc.vector.tensor_mul(area1[:, :, 0], a_side[:, :, 0], a_side[:, :, 1])
+
+        tgt_t = psum.tile([P, HALVES, ROWS], F32, name="tgt_t", tag="bank0")
+        for h in range(HALVES):
+            nc.tensor.matmul(
+                tgt_t[:, h, :], tgt_rows[:, h * P : (h + 1) * P], ident[0:ROWS, 0:ROWS], start=True, stop=True
+            )
+
+        tgt_points_last = tgt_t[:].rearrange("p h (k d) -> p d h k", d=XY)
+        b_hi = held.tile([P, XY, HALVES], F32, name="b_hi")
+        b_lo = held.tile([P, XY, HALVES], F32, name="b_lo")
+        b_side = held.tile([P, XY, HALVES], F32, name="b_side")
+        area2 = held.tile([P, HALVES], F32, name="area2")
+        tgt_sum = held.tile([P, HALVES], F32, name="tgt_sum")
+        nc.vector.tensor_reduce(out=b_hi[:], in_=tgt_points_last, axis=X, op=ALU.max)
+        nc.vector.tensor_reduce(out=b_lo[:], in_=tgt_points_last, axis=X, op=ALU.min)
+        nc.vector.tensor_reduce(out=tgt_sum[:], in_=tgt_t[:], axis=X, op=ALU.add)
+        nc.vector.tensor_sub(b_side[:], b_hi[:], b_lo[:])
+        nc.vector.tensor_mul(area2[:], b_side[:, 0, :], b_side[:, 1, :])
         nc.vector.tensor_reduce(out=pred_sum[:], in_=pred[:], axis=X, op=ALU.add)
-        nc.vector.tensor_scalar_mul(pred_term[:], pred_sum[:], -0.625)
-
-        offloaded_terms = psum.tile([P, BLOCKS * N], F32, name="offloaded_terms")
-        given_sum = [None for b in range(BLOCKS)]
-        left_sum = [None for b in range(BLOCKS)]
-
-        def offload_term(c):
-            term = held.tile([P, BLOCKS * N], F32, name=f"term{c}")
-            for b in range(BLOCKS):
-                nc.scalar.activation(
-                    out=block(term, b), in_=tgt[:, reversed_partner(c), :], func=FN.Relu,
-                    bias=neg_pred[:, b, c : c + 1], scale=1.0,
-                )
-            if c == 0:
-                for b in range(BLOCKS):
-                    left_sum[b] = block(term, b)
-            else:
-                nc.tensor.matmul(offloaded_terms[:], ident[:], term[:], start=(c == 1), stop=False)
-
-        def add_term(sums, label, c, row):
-            longer = held.tile([P, BLOCKS * N], F32, name=f"{label}{c}")
-            for b in range(BLOCKS):
-                if sums[b] is None:
-                    nc.vector.tensor_scalar_max(block(longer, b), tgt[:, row, :], pred[:, b, c : c + 1])
-                else:
-                    nc.vector.scalar_tensor_tensor(
-                        out=block(longer, b), in0=tgt[:, row, :], scalar=pred[:, b, c : c + 1],
-                        in1=sums[b], op0=ALU.max, op1=ALU.add,
-                    )
-                sums[b] = block(longer, b)
-            return longer
-
-        def use_row(row):
-            add_term(given_sum, "given", row, row)
-            if reversed_partner(row) >= OFFLOADED:
-                return add_term(left_sum, "left", reversed_partner(row), row)
-
-        offload_term(0)
-        use_row(0)
-        use_row(1)
+        nc.vector.tensor_scalar_mul(pred_term[:], pred_sum[:], 0.625)
 
         def spread(columns, coords, name):
-            row = psum.tile([P, coords * N], F32, name=name)
+            row = psum.tile([P, coords, Q], F32, name=name)
             for d in range(coords):
-                for h in range(HALVES):
-                    first = d * N + h * P
+                for b in range(BLOCKS):
                     nc.tensor.transpose(
-                        row[:, first : first + P], columns[:, d, h : h + 1].to_broadcast([P, P]), ident[:]
+                        row[:, d, b * P : (b + 1) * P], columns[:, b, d : d + 1].to_broadcast([P, P]), ident[:]
                     )
             return row
 
-        b_hi = spread(col_hi, XY, "b_hi")
-        b_lo = spread(col_lo, XY, "b_lo")
-        b_side = spread(col_side, XY, "b_side")
-        area2 = spread(col_area, 1, "area2")
+        a_hi_rows = spread(a_hi, XY, "a_hi_rows")
+        a_lo_rows = spread(a_lo, XY, "a_lo_rows")
+        a_side_rows = spread(a_side, XY, "a_side_rows")
+        area1_row = spread(area1, 1, "area1_row")
 
-        offload_term(1)
+        def per_side(name):
+            return held.tile([P, HALVES, XY, Q], F32, name=name)
+
+        def per_half(name):
+            return held.tile([P, HALVES, Q], F32, name=name)
+
+
+        sides = [(h, d) for h in range(HALVES) for d in range(XY)]
+        above, lost, overlap, extent = (per_side(s) for s in ("above", "lost", "overlap", "extent"))
+        for h, d in sides:
+            nc.scalar.activation(
+                out=above[:, h, d, :], in_=a_hi_rows[:, d, :], func=FN.Relu, bias=b_hi[:, d, h : h + 1], scale=-1.0
+            )
+        for h, d in sides:
+            nc.vector.scalar_tensor_tensor(
+                out=lost[:, h, d, :], in0=a_lo_rows[:, d, :], scalar=b_lo[:, d, h : h + 1],
+                in1=above[:, h, d, :], op0=ALU.max, op1=ALU.add,
+            )
+        for h, d in sides:
+            nc.scalar.activation(
+                out=overlap[:, h, d, :], in_=lost[:, h, d, :], func=FN.Relu, bias=b_hi[:, d, h : h + 1], scale=-1.0
+            )
+        for h, d in sides:
+            nc.vector.scalar_tensor_tensor(
+                out=extent[:, h, d, :], in0=lost[:, h, d, :], scalar=b_lo[:, d, h : h + 1],
+                in1=a_side_rows[:, d, :], op0=ALU.subtract, op1=ALU.add,
+            )
 
         expd = held.tile([P, BLOCKS, S], F32, name="expd")
         total = held.tile([P, BLOCKS], F32, name="total")
@@ -163,17 +148,57 @@ def tile_hungarianmatcherpolyline_kernel(tc, logits, pred_poly, tgt_poly, offs, 
                 out=expd[:, b, :], in_=scores[:, b, :], func=FN.Exp, accum_out=total[:, b : b + 1],
             )
 
-        use_row(6)
-        use_row(7)
-        offload_term(2)
-        offload_term(3)
-        use_row(4)
-        use_row(5)
-        offload_term(4)
-        use_row(2)
-        left_total = use_row(3)
-        nc.tensor.matmul(offloaded_terms[:], ident[:], left_total[:], start=False, stop=True)
+        given_sum = psum.tile([P, HALVES * Q], F32, name="given_sum")
+        reversed_sum = psum.tile([P, HALVES * Q], F32, name="reversed_sum")
 
+        def add_term(total_flipped, c, row, by_scalar, start, stop):
+            term = held.tile([P, BLOCKS * N], F32, name=f"term{c}_{row}")
+            for b in range(BLOCKS):
+                if by_scalar:
+                    nc.scalar.activation(
+                        out=term[:, b * N : (b + 1) * N], in_=tgt[:, row, :], func=FN.Relu,
+                        bias=neg_pred[:, b, c : c + 1], scale=1.0,
+                    )
+                else:
+                    nc.vector.tensor_scalar(
+                        out=term[:, b * N : (b + 1) * N], in0=tgt[:, row, :], scalar1=pred[:, b, c : c + 1],
+                        scalar2=0.0, op0=ALU.subtract, op1=ALU.max,
+                    )
+            squares = [(b, h) for b in range(BLOCKS) for h in range(HALVES)]
+            for b, h in squares:
+                add_flipped(
+                    total_flipped, h * Q + b * P, term, slice(b * N + h * P, b * N + (h + 1) * P),
+                    start=start and (b, h) == squares[0], stop=stop and (b, h) == squares[-1],
+                )
+
+        for i, row in enumerate(ROW_ORDER):
+            add_term(given_sum, row, row, False, i == 0, i == ROWS - 1)
+            add_term(reversed_sum, reversed_partner(row), row, i < SCALAR_ROWS, i == 0, i == ROWS - 1)
+
+        hull, hull_root, hull_inv = (per_half(f"hull{s}") for s in ("", "_root", "_inv"))
+        union, union_root, union_inv = (per_half(f"union{s}") for s in ("", "_root", "_inv"))
+        neg_inter = per_half("neg_inter")
+        excess = per_half("excess")
+        for h in range(HALVES):
+            nc.vector.tensor_mul(hull[:, h, :], extent[:, h, 0, :], extent[:, h, 1, :])
+        for h in range(HALVES):
+            nc.vector.scalar_tensor_tensor(
+                out=neg_inter[:, h, :], in0=overlap[:, h, 0, :], scalar=-1.0, in1=overlap[:, h, 1, :],
+                op0=ALU.mult, op1=ALU.mult,
+            )
+        for h in range(HALVES):
+            nc.vector.scalar_tensor_tensor(
+                out=union[:, h, :], in0=area1_row[:, 0, :], scalar=area2[:, h : h + 1], in1=neg_inter[:, h, :],
+                op0=ALU.add, op1=ALU.add,
+            )
+
+        tgt_sum_row = psum.tile([P, N], F32, name="tgt_sum_row", tag="bank1")
+        for h in range(HALVES):
+            nc.tensor.transpose(
+                tgt_sum_row[:, h * P : (h + 1) * P], tgt_sum[:, h : h + 1].to_broadcast([P, P]), ident[:]
+            )
+        tgt_term = held.tile([P, N], F32, name="tgt_term")
+        nc.scalar.activation(out=tgt_term[:], in_=tgt_sum_row[:], func=FN.Copy, scale=-0.625)
         inv_total = held.tile([P, BLOCKS], F32, name="inv_total")
         neg_prob = [held.tile([P, S], F32, name=f"neg_prob{b}") for b in range(BLOCKS)]
         picked = [held.tile([P, N], F32, name=f"picked{b}") for b in range(BLOCKS)]
@@ -186,93 +211,60 @@ def tile_hungarianmatcherpolyline_kernel(tc, logits, pred_poly, tgt_poly, offs, 
         for b in range(BLOCKS):
             nc.vector.tensor_tensor(picked[b][:], neg_prob[b][:].indirect(offsets[:]), tgt_term[:], ALU.add)
 
-        above = held.tile([P, BLOCKS, XY * N], F32, name="above")
-        lost = held.tile([P, BLOCKS, XY * N], F32, name="lost")
-        overlap = held.tile([P, BLOCKS, XY * N], F32, name="overlap")
-        extent = held.tile([P, BLOCKS, XY * N], F32, name="extent")
-        x_cols, y_cols = slice(0, N), slice(N, XY * N)
-        sides = [(b, d, slice(d * N, (d + 1) * N)) for b in range(BLOCKS) for d in range(XY)]
+        flipped_back = [psum.tile([P, N], F32, name=f"flipped_back{b}", tag=f"bank{b}") for b in range(BLOCKS)]
 
-        def per_block(name):
-            return held.tile([P, BLOCKS, N], F32, name=name)
-
-        hull, hull_root, hull_inv = (per_block(f"hull{s}") for s in ("", "_root", "_inv"))
-        union, union_root, union_inv = (per_block(f"union{s}") for s in ("", "_root", "_inv"))
-        inter = per_block("inter")
-        excess = per_block("excess")
-
-        for b, d, cols in sides:
-            nc.scalar.activation(
-                out=above[:, b, cols], in_=b_hi[:, cols], func=FN.Relu, bias=a_hi[:, b, d : d + 1], scale=-1.0
-            )
-        for b, d, cols in sides:
-            nc.vector.scalar_tensor_tensor(
-                out=lost[:, b, cols], in0=b_lo[:, cols], scalar=a_lo[:, b, d : d + 1],
-                in1=above[:, b, cols], op0=ALU.max, op1=ALU.add,
-            )
-        for b, d, cols in sides:
-            nc.scalar.activation(
-                out=overlap[:, b, cols], in_=lost[:, b, cols], func=FN.Relu, bias=a_hi[:, b, d : d + 1], scale=-1.0
-            )
-        for b, d, cols in sides:
-            nc.vector.scalar_tensor_tensor(
-                out=extent[:, b, cols], in0=lost[:, b, cols], scalar=a_lo[:, b, d : d + 1],
-                in1=b_side[:, cols], op0=ALU.subtract, op1=ALU.add,
-            )
-        for b in range(BLOCKS):
-            nc.vector.tensor_mul(hull[:, b, :], extent[:, b, x_cols], extent[:, b, y_cols])
-        for b in range(BLOCKS):
-            nc.vector.tensor_mul(inter[:, b, :], overlap[:, b, x_cols], overlap[:, b, y_cols])
-        for b in range(BLOCKS):
-            nc.vector.scalar_tensor_tensor(
-                out=union[:, b, :], in0=area2[:], scalar=area1[:, b : b + 1], in1=inter[:, b, :],
-                op0=ALU.add, op1=ALU.subtract,
-            )
+        def add_back(part, start, stop):
+            for h in range(HALVES):
+                for b in range(BLOCKS):
+                    add_flipped(
+                        flipped_back[b], h * P, part[:, h, :], slice(b * P, (b + 1) * P),
+                        start=start and h == 0, stop=stop and h == HALVES - 1,
+                    )
 
         nc.scalar.activation(out=warmed[:], in_=total[:, BLOCKS - 1 : BLOCKS], func=FN.Abs_reciprocal_sqrt)
 
-        def invert(area, root, inv):
-            for b in range(BLOCKS):
-                nc.scalar.activation(out=root[:, b, :], in_=area[:, b, :], func=FN.Abs_reciprocal_sqrt)
-            for b in range(BLOCKS):
-                nc.scalar.activation(out=inv[:, b, :], in_=root[:, b, :], func=FN.Square)
+        reversed_scaled = per_half("reversed_scaled")
+        best = per_half("best")
+        for h in range(HALVES):
+            nc.scalar.activation(
+                out=reversed_scaled[:, h, :], in_=reversed_sum[:, h * Q : (h + 1) * Q], func=FN.Copy, scale=1.25
+            )
+        for h in range(HALVES):
+            nc.vector.scalar_tensor_tensor(
+                out=best[:, h, :], in0=given_sum[:, h * Q : (h + 1) * Q], scalar=1.25, in1=reversed_scaled[:, h, :],
+                op0=ALU.mult, op1=ALU.min,
+            )
 
+        def invert(area, root, inv):
+            for h in range(HALVES):
+                nc.scalar.activation(out=root[:, h, :], in_=area[:, h, :], func=FN.Abs_reciprocal_sqrt)
+            for h in range(HALVES):
+                nc.scalar.activation(out=inv[:, h, :], in_=root[:, h, :], func=FN.Square)
+
+        excess_ratio = per_half("excess_ratio")
+        neg_inter_ratio = per_half("neg_inter_ratio")
         invert(hull, hull_root, hull_inv)
         invert(union, union_root, union_inv)
-        for b in range(BLOCKS):
-            nc.vector.tensor_sub(excess[:, b, :], hull[:, b, :], union[:, b, :])
+        for h in range(HALVES):
+            nc.vector.tensor_sub(excess[:, h, :], hull[:, h, :], union[:, h, :])
+        for h in range(HALVES):
+            nc.vector.scalar_tensor_tensor(
+                out=excess_ratio[:, h, :], in0=hull_inv[:, h, :], scalar=1.0 / EPS, in1=excess[:, h, :],
+                op0=ALU.min, op1=ALU.mult,
+            )
+        add_back(excess_ratio, True, False)
+        for h in range(HALVES):
+            nc.vector.scalar_tensor_tensor(
+                out=neg_inter_ratio[:, h, :], in0=union_inv[:, h, :], scalar=1.0 / EPS, in1=neg_inter[:, h, :],
+                op0=ALU.min, op1=ALU.mult,
+            )
+        add_back(neg_inter_ratio, False, False)
+        add_back(best, False, True)
 
-        excess_ratio = per_block("excess_ratio")
-        inter_ratio = per_block("inter_ratio")
-        with_excess = per_block("with_excess")
-        all_but_inter = per_block("all_but_inter")
-        best = per_block("best")
         cost = [held.tile([P, N], F32, name=f"cost{b}") for b in range(BLOCKS)]
-        for b in range(BLOCKS):
-            nc.vector.scalar_tensor_tensor(
-                out=excess_ratio[:, b, :], in0=hull_inv[:, b, :], scalar=1.0 / EPS, in1=excess[:, b, :],
-                op0=ALU.min, op1=ALU.mult,
-            )
-        for b in range(BLOCKS):
-            nc.vector.scalar_tensor_tensor(
-                out=with_excess[:, b, :], in0=picked[b][:], scalar=pred_term[:, b : b + 1],
-                in1=excess_ratio[:, b, :], op0=ALU.add, op1=ALU.add,
-            )
-        for b in range(BLOCKS):
-            nc.vector.scalar_tensor_tensor(
-                out=best[:, b, :], in0=block(offloaded_terms, b), scalar=offloaded_sum[:, b : b + 1],
-                in1=given_sum[b], op0=ALU.add, op1=ALU.min,
-            )
-        for b in range(BLOCKS):
-            nc.vector.scalar_tensor_tensor(
-                out=all_but_inter[:, b, :], in0=best[:, b, :], scalar=1.25, in1=with_excess[:, b, :],
-                op0=ALU.mult, op1=ALU.add,
-            )
-        for b in range(BLOCKS):
-            nc.vector.scalar_tensor_tensor(
-                out=inter_ratio[:, b, :], in0=union_inv[:, b, :], scalar=1.0 / EPS, in1=inter[:, b, :],
-                op0=ALU.min, op1=ALU.mult,
-            )
         for b, queue in enumerate((nc.sync, nc.scalar)):
-            nc.vector.tensor_sub(cost[b][:], all_but_inter[:, b, :], inter_ratio[:, b, :])
+            nc.vector.scalar_tensor_tensor(
+                out=cost[b][:], in0=flipped_back[b][:], scalar=pred_term[:, b : b + 1], in1=picked[b][:],
+                op0=ALU.add, op1=ALU.add,
+            )
             queue.dma_start(out.rearrange("(p b) j -> p b j", b=BLOCKS)[:, b, :], cost[b][:])

@@ -1,5 +1,4 @@
 import concourse.mybir as mybir
-from concourse.masks import make_identity
 
 F32 = mybir.dt.float32
 U16 = mybir.dt.uint16
@@ -8,14 +7,15 @@ FN = mybir.ActivationFunctionType
 X = mybir.AxisListType.X
 
 P = 128
+QUADRANT = 32
 Q, S, N = 256, 256, 256
 K, XY = 4, 2
 ROWS = K * XY
 BLOCKS = Q // P
 HALVES = N // P
 EPS = 1e-6
-ROW_ORDER = (6, 7, 0, 1, 4, 5, 2, 3)
-SCALAR_ROWS = 4
+ROW_ORDER = (0, 6, 7, 1, 4, 5, 2, 3)
+ROWS_BEFORE_BOXES = 3
 
 
 def reversed_partner(c):
@@ -25,14 +25,8 @@ def reversed_partner(c):
 def tile_hungarianmatcherpolyline_kernel(tc, logits, pred_poly, tgt_poly, offs, out):
     nc = tc.nc
     with tc.tile_pool(name="held", bufs=1) as held, tc.psum_pool(name="psum", bufs=1) as psum:
-        tgt_rows = held.tile([ROWS, N], F32, name="tgt_rows")
-        nc.sync.dma_start(tgt_rows[:], tgt_poly)
-
         pred = held.tile([P, BLOCKS, ROWS], F32, name="pred")
         nc.scalar.dma_start(pred[:], pred_poly.rearrange("(p b) c -> p b c", b=BLOCKS))
-
-        scores = held.tile([P, BLOCKS, S], F32, name="scores")
-        nc.sync.dma_start(scores[:], logits.rearrange("(p b) s -> p b s", b=BLOCKS))
 
         tgt = held.tile([P, ROWS, N], F32, name="tgt")
 
@@ -43,17 +37,34 @@ def tile_hungarianmatcherpolyline_kernel(tc, logits, pred_poly, tgt_poly, offs, 
                 rows.partition_broadcast(P),
             )
 
-        for d in range(XY):
-            load_rows(3 * XY + d, 1, nc.scalar)
-            load_rows(0 * XY + d, 1, nc.sync)
+        load_rows(0, 1, nc.sync)
+        load_rows(3 * XY, 1, nc.scalar)
+        tgt_rows = held.tile([ROWS, N], F32, name="tgt_rows")
+        nc.sync.dma_start(tgt_rows[:], tgt_poly)
+        scores = held.tile([P, BLOCKS, S], F32, name="scores")
+        nc.sync.dma_start(scores[:], logits.rearrange("(p b) s -> p b s", b=BLOCKS))
+        load_rows(3 * XY + 1, 1, nc.scalar)
+        load_rows(1, 1, nc.sync)
         load_rows(2 * XY, XY, nc.scalar)
         load_rows(1 * XY, XY, nc.sync)
 
         offsets = held.tile([P, N // 16], U16, name="offsets")
         nc.sync.dma_start(offsets[:], offs)
 
+        column_index = held.tile([P, QUADRANT], F32, name="column_index", align_bytes=64)
+        partition_index = held.tile([P, QUADRANT], F32, name="partition_index", align_bytes=64)
         ident = held.tile([P, P], F32, name="ident")
-        make_identity(nc, ident[:])
+        nc.vector.memset(column_index[:, 0:1], 0.0)
+        for width in (1, 2, 4, 8, 16):
+            nc.vector.tensor_scalar_add(column_index[:, width : 2 * width], column_index[:, 0:width], float(width))
+        nc.vector.transpose(partition_index[:], column_index[:])
+        nc.vector.memset(ident[:], 0.0)
+        for first in range(0, P, QUADRANT):
+            block = slice(first, first + QUADRANT)
+            nc.vector.tensor_single_scalar(
+                out=ident[block, block], in_=column_index[block, :], scalar=partition_index[block, 0:1],
+                op=ALU.is_equal,
+            )
         dummy = held.tile([P, 1], F32, name="dummy")
         nc.vector.memset(dummy[:], 0.0)
         warmed = held.tile([P, 1], F32, name="warmed")
@@ -65,39 +76,24 @@ def tile_hungarianmatcherpolyline_kernel(tc, logits, pred_poly, tgt_poly, offs, 
                 is_transpose=True, start=start, stop=stop,
             )
 
+        def per_side(name):
+            return held.tile([P, HALVES, XY, Q], F32, name=name)
+
+        def per_half(name):
+            return held.tile([P, HALVES, Q], F32, name=name)
+
+
         neg_pred = held.tile([P, BLOCKS, ROWS], F32, name="neg_pred")
         a_hi = held.tile([P, BLOCKS, XY], F32, name="a_hi")
         a_lo = held.tile([P, BLOCKS, XY], F32, name="a_lo")
         a_side = held.tile([P, BLOCKS, XY], F32, name="a_side")
         area1 = held.tile([P, BLOCKS, 1], F32, name="area1")
-        pred_sum = held.tile([P, BLOCKS], F32, name="pred_sum")
-        pred_term = held.tile([P, BLOCKS], F32, name="pred_term")
         pred_points_last = pred[:].rearrange("p b (k d) -> p b d k", d=XY)
-        nc.vector.tensor_scalar_mul(neg_pred[:], pred[:], -1.0)
         nc.vector.tensor_reduce(out=a_hi[:], in_=pred_points_last, axis=X, op=ALU.max)
         nc.vector.tensor_reduce(out=a_lo[:], in_=pred_points_last, axis=X, op=ALU.min)
+        nc.vector.tensor_scalar_mul(neg_pred[:], pred[:], -1.0)
         nc.vector.tensor_sub(a_side[:], a_hi[:], a_lo[:])
         nc.vector.tensor_mul(area1[:, :, 0], a_side[:, :, 0], a_side[:, :, 1])
-
-        tgt_t = psum.tile([P, HALVES, ROWS], F32, name="tgt_t", tag="bank0")
-        for h in range(HALVES):
-            nc.tensor.matmul(
-                tgt_t[:, h, :], tgt_rows[:, h * P : (h + 1) * P], ident[0:ROWS, 0:ROWS], start=True, stop=True
-            )
-
-        tgt_points_last = tgt_t[:].rearrange("p h (k d) -> p d h k", d=XY)
-        b_hi = held.tile([P, XY, HALVES], F32, name="b_hi")
-        b_lo = held.tile([P, XY, HALVES], F32, name="b_lo")
-        b_side = held.tile([P, XY, HALVES], F32, name="b_side")
-        area2 = held.tile([P, HALVES], F32, name="area2")
-        tgt_sum = held.tile([P, HALVES], F32, name="tgt_sum")
-        nc.vector.tensor_reduce(out=b_hi[:], in_=tgt_points_last, axis=X, op=ALU.max)
-        nc.vector.tensor_reduce(out=b_lo[:], in_=tgt_points_last, axis=X, op=ALU.min)
-        nc.vector.tensor_reduce(out=tgt_sum[:], in_=tgt_t[:], axis=X, op=ALU.add)
-        nc.vector.tensor_sub(b_side[:], b_hi[:], b_lo[:])
-        nc.vector.tensor_mul(area2[:], b_side[:, 0, :], b_side[:, 1, :])
-        nc.vector.tensor_reduce(out=pred_sum[:], in_=pred[:], axis=X, op=ALU.add)
-        nc.vector.tensor_scalar_mul(pred_term[:], pred_sum[:], 0.625)
 
         def spread(columns, coords, name):
             row = psum.tile([P, coords, Q], F32, name=name)
@@ -109,44 +105,14 @@ def tile_hungarianmatcherpolyline_kernel(tc, logits, pred_poly, tgt_poly, offs, 
             return row
 
         a_hi_rows = spread(a_hi, XY, "a_hi_rows")
+        tgt_t = psum.tile([P, HALVES, ROWS], F32, name="tgt_t", tag="bank0")
+        for h in range(HALVES):
+            nc.tensor.matmul(
+                tgt_t[:, h, :], tgt_rows[:, h * P : (h + 1) * P], ident[0:ROWS, 0:ROWS], start=True, stop=True
+            )
         a_lo_rows = spread(a_lo, XY, "a_lo_rows")
         a_side_rows = spread(a_side, XY, "a_side_rows")
         area1_row = spread(area1, 1, "area1_row")
-
-        def per_side(name):
-            return held.tile([P, HALVES, XY, Q], F32, name=name)
-
-        def per_half(name):
-            return held.tile([P, HALVES, Q], F32, name=name)
-
-
-        sides = [(h, d) for h in range(HALVES) for d in range(XY)]
-        above, lost, overlap, extent = (per_side(s) for s in ("above", "lost", "overlap", "extent"))
-        for h, d in sides:
-            nc.scalar.activation(
-                out=above[:, h, d, :], in_=a_hi_rows[:, d, :], func=FN.Relu, bias=b_hi[:, d, h : h + 1], scale=-1.0
-            )
-        for h, d in sides:
-            nc.vector.scalar_tensor_tensor(
-                out=lost[:, h, d, :], in0=a_lo_rows[:, d, :], scalar=b_lo[:, d, h : h + 1],
-                in1=above[:, h, d, :], op0=ALU.max, op1=ALU.add,
-            )
-        for h, d in sides:
-            nc.scalar.activation(
-                out=overlap[:, h, d, :], in_=lost[:, h, d, :], func=FN.Relu, bias=b_hi[:, d, h : h + 1], scale=-1.0
-            )
-        for h, d in sides:
-            nc.vector.scalar_tensor_tensor(
-                out=extent[:, h, d, :], in0=lost[:, h, d, :], scalar=b_lo[:, d, h : h + 1],
-                in1=a_side_rows[:, d, :], op0=ALU.subtract, op1=ALU.add,
-            )
-
-        expd = held.tile([P, BLOCKS, S], F32, name="expd")
-        total = held.tile([P, BLOCKS], F32, name="total")
-        for b in range(BLOCKS):
-            nc.scalar.activation(
-                out=expd[:, b, :], in_=scores[:, b, :], func=FN.Exp, accum_out=total[:, b : b + 1],
-            )
 
         given_sum = psum.tile([P, HALVES * Q], F32, name="given_sum")
         reversed_sum = psum.tile([P, HALVES * Q], F32, name="reversed_sum")
@@ -171,14 +137,67 @@ def tile_hungarianmatcherpolyline_kernel(tc, logits, pred_poly, tgt_poly, offs, 
                     start=start and (b, h) == squares[0], stop=stop and (b, h) == squares[-1],
                 )
 
-        for i, row in enumerate(ROW_ORDER):
+        def add_row_terms(i):
+            row = ROW_ORDER[i]
             add_term(given_sum, row, row, False, i == 0, i == ROWS - 1)
-            add_term(reversed_sum, reversed_partner(row), row, i < SCALAR_ROWS, i == 0, i == ROWS - 1)
+            add_term(reversed_sum, reversed_partner(row), row, i % 2 == 1, i == 0, i == ROWS - 1)
 
+        for i in range(ROWS_BEFORE_BOXES):
+            add_row_terms(i)
+
+        expd = held.tile([P, BLOCKS, S], F32, name="expd")
+        total = held.tile([P, BLOCKS], F32, name="total")
+        for b in range(BLOCKS):
+            nc.scalar.activation(
+                out=expd[:, b, :], in_=scores[:, b, :], func=FN.Exp, accum_out=total[:, b : b + 1],
+            )
+        nc.scalar.activation(out=warmed[:], in_=total[:, 0:1], func=FN.Abs_reciprocal_sqrt)
+
+        tgt_points_last = tgt_t[:].rearrange("p h (k d) -> p d h k", d=XY)
+        b_hi = held.tile([P, XY, HALVES], F32, name="b_hi")
+        b_lo = held.tile([P, XY, HALVES], F32, name="b_lo")
+        b_side = held.tile([P, XY, HALVES], F32, name="b_side")
+        area2 = held.tile([P, HALVES], F32, name="area2")
+        tgt_sum = held.tile([P, HALVES], F32, name="tgt_sum")
+        nc.vector.tensor_reduce(out=b_hi[:], in_=tgt_points_last, axis=X, op=ALU.max)
+        nc.vector.tensor_reduce(out=b_lo[:], in_=tgt_points_last, axis=X, op=ALU.min)
+        nc.vector.tensor_sub(b_side[:], b_hi[:], b_lo[:])
+        nc.vector.tensor_mul(area2[:], b_side[:, 0, :], b_side[:, 1, :])
+        nc.vector.tensor_reduce(out=tgt_sum[:], in_=tgt_t[:], axis=X, op=ALU.add)
+        tgt_sum_row = psum.tile([P, N], F32, name="tgt_sum_row", tag="bank1")
+        for h in range(HALVES):
+            nc.tensor.transpose(
+                tgt_sum_row[:, h * P : (h + 1) * P], tgt_sum[:, h : h + 1].to_broadcast([P, P]), ident[:]
+            )
+        tgt_term = held.tile([P, N], F32, name="tgt_term")
+        nc.scalar.activation(out=tgt_term[:], in_=tgt_sum_row[:], func=FN.Copy, scale=-0.625)
+
+        sides = [(h, d) for h in range(HALVES) for d in range(XY)]
+        above, lost, overlap, extent = (per_side(s) for s in ("above", "lost", "overlap", "extent"))
         hull, hull_root, hull_inv = (per_half(f"hull{s}") for s in ("", "_root", "_inv"))
         union, union_root, union_inv = (per_half(f"union{s}") for s in ("", "_root", "_inv"))
         neg_inter = per_half("neg_inter")
         excess = per_half("excess")
+        excess_ratio = per_half("excess_ratio")
+        neg_inter_ratio = per_half("neg_inter_ratio")
+        for h, d in sides:
+            nc.scalar.activation(
+                out=above[:, h, d, :], in_=a_hi_rows[:, d, :], func=FN.Relu, bias=b_hi[:, d, h : h + 1], scale=-1.0
+            )
+        for h, d in sides:
+            nc.vector.scalar_tensor_tensor(
+                out=lost[:, h, d, :], in0=a_lo_rows[:, d, :], scalar=b_lo[:, d, h : h + 1],
+                in1=above[:, h, d, :], op0=ALU.max, op1=ALU.add,
+            )
+        for h, d in sides:
+            nc.scalar.activation(
+                out=overlap[:, h, d, :], in_=lost[:, h, d, :], func=FN.Relu, bias=b_hi[:, d, h : h + 1], scale=-1.0
+            )
+        for h, d in sides:
+            nc.vector.scalar_tensor_tensor(
+                out=extent[:, h, d, :], in0=lost[:, h, d, :], scalar=b_lo[:, d, h : h + 1],
+                in1=a_side_rows[:, d, :], op0=ALU.subtract, op1=ALU.add,
+            )
         for h in range(HALVES):
             nc.vector.tensor_mul(hull[:, h, :], extent[:, h, 0, :], extent[:, h, 1, :])
         for h in range(HALVES):
@@ -192,37 +211,8 @@ def tile_hungarianmatcherpolyline_kernel(tc, logits, pred_poly, tgt_poly, offs, 
                 op0=ALU.add, op1=ALU.add,
             )
 
-        tgt_sum_row = psum.tile([P, N], F32, name="tgt_sum_row", tag="bank1")
-        for h in range(HALVES):
-            nc.tensor.transpose(
-                tgt_sum_row[:, h * P : (h + 1) * P], tgt_sum[:, h : h + 1].to_broadcast([P, P]), ident[:]
-            )
-        tgt_term = held.tile([P, N], F32, name="tgt_term")
-        nc.scalar.activation(out=tgt_term[:], in_=tgt_sum_row[:], func=FN.Copy, scale=-0.625)
-        inv_total = held.tile([P, BLOCKS], F32, name="inv_total")
-        neg_prob = [held.tile([P, S], F32, name=f"neg_prob{b}") for b in range(BLOCKS)]
-        picked = [held.tile([P, N], F32, name=f"picked{b}") for b in range(BLOCKS)]
-        nc.vector.reciprocal(inv_total[:], total[:])
-        for b in range(BLOCKS):
-            nc.vector.tensor_scalar(
-                out=neg_prob[b][:], in0=expd[:, b, :], scalar1=inv_total[:, b : b + 1], scalar2=-1.0,
-                op0=ALU.mult, op1=ALU.mult,
-            )
-        for b in range(BLOCKS):
-            nc.vector.tensor_tensor(picked[b][:], neg_prob[b][:].indirect(offsets[:]), tgt_term[:], ALU.add)
-
-        flipped_back = [psum.tile([P, N], F32, name=f"flipped_back{b}", tag=f"bank{b}") for b in range(BLOCKS)]
-
-        def add_back(part, start, stop):
-            for h in range(HALVES):
-                for b in range(BLOCKS):
-                    add_flipped(
-                        flipped_back[b], h * P, part[:, h, :], slice(b * P, (b + 1) * P),
-                        start=start and h == 0, stop=stop and h == HALVES - 1,
-                    )
-
-        nc.scalar.activation(out=warmed[:], in_=total[:, BLOCKS - 1 : BLOCKS], func=FN.Abs_reciprocal_sqrt)
-
+        for i in range(ROWS_BEFORE_BOXES, ROWS):
+            add_row_terms(i)
         reversed_scaled = per_half("reversed_scaled")
         best = per_half("best")
         for h in range(HALVES):
@@ -241,8 +231,6 @@ def tile_hungarianmatcherpolyline_kernel(tc, logits, pred_poly, tgt_poly, offs, 
             for h in range(HALVES):
                 nc.scalar.activation(out=inv[:, h, :], in_=root[:, h, :], func=FN.Square)
 
-        excess_ratio = per_half("excess_ratio")
-        neg_inter_ratio = per_half("neg_inter_ratio")
         invert(hull, hull_root, hull_inv)
         invert(union, union_root, union_inv)
         for h in range(HALVES):
@@ -252,14 +240,37 @@ def tile_hungarianmatcherpolyline_kernel(tc, logits, pred_poly, tgt_poly, offs, 
                 out=excess_ratio[:, h, :], in0=hull_inv[:, h, :], scalar=1.0 / EPS, in1=excess[:, h, :],
                 op0=ALU.min, op1=ALU.mult,
             )
-        add_back(excess_ratio, True, False)
         for h in range(HALVES):
             nc.vector.scalar_tensor_tensor(
                 out=neg_inter_ratio[:, h, :], in0=union_inv[:, h, :], scalar=1.0 / EPS, in1=neg_inter[:, h, :],
                 op0=ALU.min, op1=ALU.mult,
             )
-        add_back(neg_inter_ratio, False, False)
-        add_back(best, False, True)
+
+        inv_total = held.tile([P, BLOCKS], F32, name="inv_total")
+        neg_prob = [held.tile([P, S], F32, name=f"neg_prob{b}") for b in range(BLOCKS)]
+        picked = [held.tile([P, N], F32, name=f"picked{b}") for b in range(BLOCKS)]
+        nc.vector.reciprocal(inv_total[:], total[:])
+        for b in range(BLOCKS):
+            nc.vector.tensor_scalar(
+                out=neg_prob[b][:], in0=expd[:, b, :], scalar1=inv_total[:, b : b + 1], scalar2=-1.0,
+                op0=ALU.mult, op1=ALU.mult,
+            )
+        for b in range(BLOCKS):
+            nc.vector.tensor_tensor(picked[b][:], neg_prob[b][:].indirect(offsets[:]), tgt_term[:], ALU.add)
+        pred_sum = held.tile([P, BLOCKS], F32, name="pred_sum")
+        pred_term = held.tile([P, BLOCKS], F32, name="pred_term")
+        nc.vector.tensor_reduce(out=pred_sum[:], in_=pred[:], axis=X, op=ALU.add)
+        nc.vector.tensor_scalar_mul(pred_term[:], pred_sum[:], 0.625)
+
+        flipped_back = [psum.tile([P, N], F32, name=f"flipped_back{b}", tag=f"bank{b}") for b in range(BLOCKS)]
+        parts = (excess_ratio, best, neg_inter_ratio)
+        for i, part in enumerate(parts):
+            for h in range(HALVES):
+                for b in range(BLOCKS):
+                    add_flipped(
+                        flipped_back[b], h * P, part[:, h, :], slice(b * P, (b + 1) * P),
+                        start=(i == 0 and h == 0), stop=(i == len(parts) - 1 and h == HALVES - 1),
+                    )
 
         cost = [held.tile([P, N], F32, name=f"cost{b}") for b in range(BLOCKS)]
         for b, queue in enumerate((nc.sync, nc.scalar)):

@@ -14,7 +14,7 @@ ROWS = K * XY
 BLOCKS = Q // P
 HALVES = N // P
 EPS = 1e-6
-ROW_ORDER = (0, 6, 7, 1, 4, 5, 2, 3)
+ROW_ORDER = (6, 0, 7, 1, 4, 5, 2, 3)
 ROWS_BEFORE_BOXES = 3
 
 
@@ -37,12 +37,12 @@ def tile_hungarianmatcherpolyline_kernel(tc, logits, pred_poly, tgt_poly, offs, 
                 rows.partition_broadcast(P),
             )
 
-        load_rows(0, 1, nc.sync)
-        load_rows(3 * XY, 1, nc.scalar)
         tgt_rows = held.tile([ROWS, N], F32, name="tgt_rows")
         nc.sync.dma_start(tgt_rows[:], tgt_poly)
         scores = held.tile([P, BLOCKS, S], F32, name="scores")
         nc.sync.dma_start(scores[:], logits.rearrange("(p b) s -> p b s", b=BLOCKS))
+        load_rows(3 * XY, 1, nc.scalar)
+        load_rows(0, 1, nc.sync)
         load_rows(3 * XY + 1, 1, nc.scalar)
         load_rows(1, 1, nc.sync)
         load_rows(2 * XY, XY, nc.scalar)
@@ -114,6 +114,14 @@ def tile_hungarianmatcherpolyline_kernel(tc, logits, pred_poly, tgt_poly, offs, 
         a_side_rows = spread(a_side, XY, "a_side_rows")
         area1_row = spread(area1, 1, "area1_row")
 
+        expd = held.tile([P, BLOCKS, S], F32, name="expd")
+        total = held.tile([P, BLOCKS], F32, name="total")
+        for b in range(BLOCKS):
+            nc.scalar.activation(
+                out=expd[:, b, :], in_=scores[:, b, :], func=FN.Exp, accum_out=total[:, b : b + 1],
+            )
+        nc.scalar.activation(out=warmed[:], in_=total[:, 0:1], func=FN.Abs_reciprocal_sqrt)
+
         given_sum = psum.tile([P, HALVES * Q], F32, name="given_sum")
         reversed_sum = psum.tile([P, HALVES * Q], F32, name="reversed_sum")
 
@@ -144,14 +152,6 @@ def tile_hungarianmatcherpolyline_kernel(tc, logits, pred_poly, tgt_poly, offs, 
 
         for i in range(ROWS_BEFORE_BOXES):
             add_row_terms(i)
-
-        expd = held.tile([P, BLOCKS, S], F32, name="expd")
-        total = held.tile([P, BLOCKS], F32, name="total")
-        for b in range(BLOCKS):
-            nc.scalar.activation(
-                out=expd[:, b, :], in_=scores[:, b, :], func=FN.Exp, accum_out=total[:, b : b + 1],
-            )
-        nc.scalar.activation(out=warmed[:], in_=total[:, 0:1], func=FN.Abs_reciprocal_sqrt)
 
         tgt_points_last = tgt_t[:].rearrange("p h (k d) -> p d h k", d=XY)
         b_hi = held.tile([P, XY, HALVES], F32, name="b_hi")

import concourse.mybir as mybir

F32 = mybir.dt.float32
U16 = mybir.dt.uint16
ALU = mybir.AluOpType
FN = mybir.ActivationFunctionType
X = mybir.AxisListType.X

P = 128
QUADRANT = 32
Q, S, N = 256, 256, 256
K, XY = 4, 2
ROWS = K * XY
BLOCKS = Q // P
HALVES = N // P
EPS = 1e-6
ROW_ORDER = (6, 0, 7, 1, 4, 5, 2, 3)
ROWS_BEFORE_BOXES = 3


def reversed_partner(c):
    return (K - 1 - c // XY) * XY + c % XY


def tile_hungarianmatcherpolyline_kernel(tc, logits, pred_poly, tgt_poly, offs, out):
    nc = tc.nc
    with tc.tile_pool(name="held", bufs=1) as held, tc.psum_pool(name="psum", bufs=1) as psum:
        pred = held.tile([P, BLOCKS, ROWS], F32, name="pred")
        nc.scalar.dma_start(pred[:], pred_poly.rearrange("(p b) c -> p b c", b=BLOCKS))

        tgt = held.tile([P, ROWS, N], F32, name="tgt")

        def load_rows(first, count, queue):
            rows = tgt_poly[first : first + count, :].rearrange("r j -> (r j)")
            queue.dma_start(
                tgt[:].rearrange("p r j -> p (r j)")[:, first * N : (first + count) * N],
                rows.partition_broadcast(P),
            )

        tgt_rows = held.tile([ROWS, N], F32, name="tgt_rows")
        nc.sync.dma_start(tgt_rows[:], tgt_poly)
        scores = held.tile([P, BLOCKS, S], F32, name="scores")
        nc.sync.dma_start(scores[:], logits.rearrange("(p b) s -> p b s", b=BLOCKS))
        load_rows(3 * XY, 1, nc.scalar)
        load_rows(0, 1, nc.sync)
        load_rows(3 * XY + 1, 1, nc.scalar)
        load_rows(1, 1, nc.sync)
        load_rows(2 * XY, XY, nc.scalar)
        load_rows(1 * XY, XY, nc.sync)

        offsets = held.tile([P, N // 16], U16, name="offsets")
        nc.sync.dma_start(offsets[:], offs)

        column_index = held.tile([P, QUADRANT], F32, name="column_index", align_bytes=64)
        partition_index = held.tile([P, QUADRANT], F32, name="partition_index", align_bytes=64)
        ident = held.tile([P, P], F32, name="ident")
        nc.vector.memset(column_index[:, 0:1], 0.0)
        for width in (1, 2, 4, 8, 16):
            nc.vector.tensor_scalar_add(column_index[:, width : 2 * width], column_index[:, 0:width], float(width))
        nc.vector.transpose(partition_index[:], column_index[:])
        nc.vector.memset(ident[:], 0.0)
        for first in range(0, P, QUADRANT):
            block = slice(first, first + QUADRANT)
            nc.vector.tensor_single_scalar(
                out=ident[block, block], in_=column_index[block, :], scalar=partition_index[block, 0:1],
                op=ALU.is_equal,
            )
        dummy = held.tile([P, 1], F32, name="dummy")
        nc.vector.memset(dummy[:], 0.0)
        warmed = held.tile([P, 1], F32, name="warmed")
        nc.scalar.activation(out=warmed[:], in_=dummy[:], func=FN.Exp)

        def add_flipped(total, first_columns, tile, columns, start, stop):
            nc.tensor.matmul(
                total[:, first_columns : first_columns + P], tile[:, columns], ident[:],
                is_transpose=True, start=start, stop=stop,
            )

        def per_side(name):
            return held.tile([P, HALVES, XY, Q], F32, name=name)

        def per_half(name):
            return held.tile([P, HALVES, Q], F32, name=name)


        neg_pred = held.tile([P, BLOCKS, ROWS], F32, name="neg_pred")
        a_hi = held.tile([P, BLOCKS, XY], F32, name="a_hi")
        a_lo = held.tile([P, BLOCKS, XY], F32, name="a_lo")
        a_side = held.tile([P, BLOCKS, XY], F32, name="a_side")
        area1 = held.tile([P, BLOCKS, 1], F32, name="area1")
        pred_points_last = pred[:].rearrange("p b (k d) -> p b d k", d=XY)
        nc.vector.tensor_reduce(out=a_hi[:], in_=pred_points_last, axis=X, op=ALU.max)
        nc.vector.tensor_reduce(out=a_lo[:], in_=pred_points_last, axis=X, op=ALU.min)
        nc.vector.tensor_scalar_mul(neg_pred[:], pred[:], -1.0)
        nc.vector.tensor_sub(a_side[:], a_hi[:], a_lo[:])
        nc.vector.tensor_mul(area1[:, :, 0], a_side[:, :, 0], a_side[:, :, 1])

        def spread(columns, coords, name):
            row = psum.tile([P, coords, Q], F32, name=name)
            for d in range(coords):
                for b in range(BLOCKS):
                    nc.tensor.transpose(
                        row[:, d, b * P : (b + 1) * P], columns[:, b, d : d + 1].to_broadcast([P, P]), ident[:]
                    )
            return row

        a_hi_rows = spread(a_hi, XY, "a_hi_rows")
        tgt_t = psum.tile([P, HALVES, ROWS], F32, name="tgt_t", tag="bank0")
        for h in range(HALVES):
            nc.tensor.matmul(
                tgt_t[:, h, :], tgt_rows[:, h * P : (h + 1) * P], ident[0:ROWS, 0:ROWS], start=True, stop=True
            )
        a_lo_rows = spread(a_lo, XY, "a_lo_rows")
        a_side_rows = spread(a_side, XY, "a_side_rows")
        area1_row = spread(area1, 1, "area1_row")

        expd = held.tile([P, BLOCKS, S], F32, name="expd")
        total = held.tile([P, BLOCKS], F32, name="total")
        for b in range(BLOCKS):
            nc.scalar.activation(
                out=expd[:, b, :], in_=scores[:, b, :], func=FN.Exp, accum_out=total[:, b : b + 1],
            )
        nc.scalar.activation(out=warmed[:], in_=total[:, 0:1], func=FN.Abs_reciprocal_sqrt)

        given_sum = psum.tile([P, HALVES * Q], F32, name="given_sum")
        reversed_sum = psum.tile([P, HALVES * Q], F32, name="reversed_sum")

        def add_term(total_flipped, c, row, by_scalar, start, stop):
            term = held.tile([P, BLOCKS * N], F32, name=f"term{c}_{row}")
            for b in range(BLOCKS):
                if by_scalar:
                    nc.scalar.activation(
                        out=term[:, b * N : (b + 1) * N], in_=tgt[:, row, :], func=FN.Relu,
                        bias=neg_pred[:, b, c : c + 1], scale=1.0,
                    )
                else:
                    nc.vector.tensor_scalar(
                        out=term[:, b * N : (b + 1) * N], in0=tgt[:, row, :], scalar1=pred[:, b, c : c + 1],
                        scalar2=0.0, op0=ALU.subtract, op1=ALU.max,
                    )
            squares = [(b, h) for b in range(BLOCKS) for h in range(HALVES)]
            for b, h in squares:
                add_flipped(
                    total_flipped, h * Q + b * P, term, slice(b * N + h * P, b * N + (h + 1) * P),
                    start=start and (b, h) == squares[0], stop=stop and (b, h) == squares[-1],
                )

        def add_row_terms(i):
            row = ROW_ORDER[i]
            add_term(given_sum, row, row, False, i == 0, i == ROWS - 1)
            add_term(reversed_sum, reversed_partner(row), row, i % 2 == 1, i == 0, i == ROWS - 1)

        for i in range(ROWS_BEFORE_BOXES):
            add_row_terms(i)

        tgt_points_last = tgt_t[:].rearrange("p h (k d) -> p d h k", d=XY)
        b_hi = held.tile([P, XY, HALVES], F32, name="b_hi")
        b_lo = held.tile([P, XY, HALVES], F32, name="b_lo")
        b_side = held.tile([P, XY, HALVES], F32, name="b_side")
        area2 = held.tile([P, HALVES], F32, name="area2")
        tgt_sum = held.tile([P, HALVES], F32, name="tgt_sum")
        nc.vector.tensor_reduce(out=b_hi[:], in_=tgt_points_last, axis=X, op=ALU.max)
        nc.vector.tensor_reduce(out=b_lo[:], in_=tgt_points_last, axis=X, op=ALU.min)
        nc.vector.tensor_sub(b_side[:], b_hi[:], b_lo[:])
        nc.vector.tensor_mul(area2[:], b_side[:, 0, :], b_side[:, 1, :])
        nc.vector.tensor_reduce(out=tgt_sum[:], in_=tgt_t[:], axis=X, op=ALU.add)
        tgt_sum_row = psum.tile([P, N], F32, name="tgt_sum_row", tag="bank1")
        for h in range(HALVES):
            nc.tensor.transpose(
                tgt_sum_row[:, h * P : (h + 1) * P], tgt_sum[:, h : h + 1].to_broadcast([P, P]), ident[:]
            )
        tgt_term = held.tile([P, N], F32, name="tgt_term")
        nc.scalar.activation(out=tgt_term[:], in_=tgt_sum_row[:], func=FN.Copy, scale=-0.625)

        sides = [(h, d) for h in range(HALVES) for d in range(XY)]
        above, lost, overlap, extent = (per_side(s) for s in ("above", "lost", "overlap", "extent"))
        hull, hull_root, hull_inv = (per_half(f"hull{s}") for s in ("", "_root", "_inv"))
        union, union_root, union_inv = (per_half(f"union{s}") for s in ("", "_root", "_inv"))
        neg_inter = per_half("neg_inter")
        excess = per_half("excess")
        excess_ratio = per_half("excess_ratio")
        neg_inter_ratio = per_half("neg_inter_ratio")
        for h, d in sides:
            nc.scalar.activation(
                out=above[:, h, d, :], in_=a_hi_rows[:, d, :], func=FN.Relu, bias=b_hi[:, d, h : h + 1], scale=-1.0
            )
        for h, d in sides:
            nc.vector.scalar_tensor_tensor(
                out=lost[:, h, d, :], in0=a_lo_rows[:, d, :], scalar=b_lo[:, d, h : h + 1],
                in1=above[:, h, d, :], op0=ALU.max, op1=ALU.add,
            )
        for h, d in sides:
            nc.scalar.activation(
                out=overlap[:, h, d, :], in_=lost[:, h, d, :], func=FN.Relu, bias=b_hi[:, d, h : h + 1], scale=-1.0
            )
        for h, d in sides:
            nc.vector.scalar_tensor_tensor(
                out=extent[:, h, d, :], in0=lost[:, h, d, :], scalar=b_lo[:, d, h : h + 1],
                in1=a_side_rows[:, d, :], op0=ALU.subtract, op1=ALU.add,
            )
        for h in range(HALVES):
            nc.vector.tensor_mul(hull[:, h, :], extent[:, h, 0, :], extent[:, h, 1, :])
        for h in range(HALVES):
            nc.vector.scalar_tensor_tensor(
                out=neg_inter[:, h, :], in0=overlap[:, h, 0, :], scalar=-1.0, in1=overlap[:, h, 1, :],
                op0=ALU.mult, op1=ALU.mult,
            )
        for h in range(HALVES):
            nc.vector.scalar_tensor_tensor(
                out=union[:, h, :], in0=area1_row[:, 0, :], scalar=area2[:, h : h + 1], in1=neg_inter[:, h, :],
                op0=ALU.add, op1=ALU.add,
            )

        for i in range(ROWS_BEFORE_BOXES, ROWS):
            add_row_terms(i)
        reversed_scaled = per_half("reversed_scaled")
        best = per_half("best")
        for h in range(HALVES):
            nc.scalar.activation(
                out=reversed_scaled[:, h, :], in_=reversed_sum[:, h * Q : (h + 1) * Q], func=FN.Copy, scale=1.25
            )
        for h in range(HALVES):
            nc.vector.scalar_tensor_tensor(
                out=best[:, h, :], in0=given_sum[:, h * Q : (h + 1) * Q], scalar=1.25, in1=reversed_scaled[:, h, :],
                op0=ALU.mult, op1=ALU.min,
            )

        def invert(area, root, inv):
            for h in range(HALVES):
                nc.scalar.activation(out=root[:, h, :], in_=area[:, h, :], func=FN.Abs_reciprocal_sqrt)
            for h in range(HALVES):
                nc.scalar.activation(out=inv[:, h, :], in_=root[:, h, :], func=FN.Square)

        invert(hull, hull_root, hull_inv)
        invert(union, union_root, union_inv)
        for h in range(HALVES):
            nc.vector.tensor_sub(excess[:, h, :], hull[:, h, :], union[:, h, :])
        for h in range(HALVES):
            nc.vector.scalar_tensor_tensor(
                out=excess_ratio[:, h, :], in0=hull_inv[:, h, :], scalar=1.0 / EPS, in1=excess[:, h, :],
                op0=ALU.min, op1=ALU.mult,
            )
        for h in range(HALVES):
            nc.vector.scalar_tensor_tensor(
                out=neg_inter_ratio[:, h, :], in0=union_inv[:, h, :], scalar=1.0 / EPS, in1=neg_inter[:, h, :],
                op0=ALU.min, op1=ALU.mult,
            )

        inv_total = held.tile([P, BLOCKS], F32, name="inv_total")
        neg_prob = [held.tile([P, S], F32, name=f"neg_prob{b}") for b in range(BLOCKS)]
        picked = [held.tile([P, N], F32, name=f"picked{b}") for b in range(BLOCKS)]
        nc.vector.reciprocal(inv_total[:], total[:])
        for b in range(BLOCKS):
            nc.vector.tensor_scalar(
                out=neg_prob[b][:], in0=expd[:, b, :], scalar1=inv_total[:, b : b + 1], scalar2=-1.0,
                op0=ALU.mult, op1=ALU.mult,
            )
        for b in range(BLOCKS):
            nc.vector.tensor_tensor(picked[b][:], neg_prob[b][:].indirect(offsets[:]), tgt_term[:], ALU.add)
        pred_sum = held.tile([P, BLOCKS], F32, name="pred_sum")
        pred_term = held.tile([P, BLOCKS], F32, name="pred_term")
        nc.vector.tensor_reduce(out=pred_sum[:], in_=pred[:], axis=X, op=ALU.add)
        nc.vector.tensor_scalar_mul(pred_term[:], pred_sum[:], 0.625)

        flipped_back = [psum.tile([P, N], F32, name=f"flipped_back{b}", tag=f"bank{b}") for b in range(BLOCKS)]
        parts = (excess_ratio, best, neg_inter_ratio)
        for i, part in enumerate(parts):
            for h in range(HALVES):
                for b in range(BLOCKS):
                    add_flipped(
                        flipped_back[b], h * P, part[:, h, :], slice(b * P, (b + 1) * P),
                        start=(i == 0 and h == 0), stop=(i == len(parts) - 1 and h == HALVES - 1),
                    )

        cost = [held.tile([P, N], F32, name=f"cost{b}") for b in range(BLOCKS)]
        for b, queue in enumerate((nc.sync, nc.scalar)):
            nc.vector.scalar_tensor_tensor(
                out=cost[b][:], in0=flipped_back[b][:], scalar=pred_term[:, b : b + 1], in1=picked[b][:],
                op0=ALU.add, op1=ALU.add,
            )
            queue.dma_start(out.rearrange("(p b) j -> p b j", b=BLOCKS)[:, b, :], cost[b][:])
